import numpy as np
import ml_dtypes


def mxq(x, axis, fmt="e4m3"):
    dtype, down = {"e4m3": (ml_dtypes.float8_e4m3fn, 7), "e5m2": (ml_dtypes.float8_e5m2, 14)}[fmt]
    v = np.moveaxis(np.asarray(x, np.float32).astype(ml_dtypes.bfloat16).astype(np.float64), axis, -1)
    blocks = v.reshape(v.shape[:-1] + (-1, 32))
    amax = np.abs(blocks).max(-1, keepdims=True)
    byte = np.maximum(np.where(amax > 0, np.frexp(amax)[1] - 1 + 127, 0) - down, 1)
    scale = np.exp2(byte - 127.0)
    codes = (blocks / scale).astype(np.float32).astype(dtype).astype(np.float64)
    return np.moveaxis((codes * scale).reshape(v.shape), -1, axis)


WIDE = False


def mx_kscale(k):
    if not WIDE:
        return np.ones(k)
    levels = np.array([10, -10, 5, -5, 0])
    if k % 512:
        return np.exp2(np.random.permutation(np.resize(levels, k // 32))).repeat(32)
    a = np.empty((k // 512, 16))
    for p in range(k // 512):
        a[p, :8] = np.random.permutation(np.resize(levels, 8))
        for g in range(8):
            far = levels[np.abs(levels - a[p, g]) >= 10]
            a[p, g + 8] = far[np.random.randint(len(far))]
    return np.exp2(a.ravel()).repeat(32)


BF16 = ml_dtypes.bfloat16


def bf(x):
    return np.asarray(x, np.float32).astype(BF16)


def f64(x):
    return np.asarray(x).astype(np.float64)


N, C_IN, C_OUT, C_DGRAM, C_AA, C_ESM = 64, 512, 1024, 39, 22, 1280
LN_EPS = 1e-5


def layer_norm(x, g, b):
    mu = x.mean(-1, keepdims=True)
    var = x.var(-1, keepdims=True)
    return (x - mu) * (1.0 / np.sqrt(var + LN_EPS)) * g + b


def setup_inputs():
    rn, ru = np.random.standard_normal, np.random.uniform
    s = mx_kscale(C_IN)

    def vec():
        return bf(rn(C_OUT) * 0.1)

    def row():
        return bf(rn(C_OUT)[None, :])

    return {
        "act_dgram": bf(rn((N, N, C_OUT)) * 0.2),
        "aa_proj1": bf(rn((N, C_OUT)) * 0.6),
        "aa_proj2": bf(rn((N, C_OUT)) * 0.6),
        "esm_proj1": bf(rn((N, C_OUT))),
        "esm_proj2": bf(rn((N, C_OUT))),
        "query_embedding": bf(rn((N, N, C_IN)) * (0.5 + 1.5 * ru(size=(N, N)))[..., None] + rn((N, N))[..., None]),
        "pseudo_beta_mask": bf(ru(size=N)),
        "backbone_mask": bf(ru(size=N)),
        "multichain_mask_2d": bf(ru(size=(N, N))),
        "unit_x": bf(rn((N, N))),
        "unit_y": bf(rn((N, N))),
        "unit_z": bf(rn((N, N))),
        "ln_g": bf((1.0 + 0.1 * rn(C_IN)) * s),
        "ln_b": bf(0.1 * rn(C_IN) * s),
        "w_q": bf(rn((C_IN, C_OUT)) / np.sqrt(C_IN) / s[:, None]),
        "b_q": vec(),
        "w_pbm": row(), "b_pbm": vec(),
        "w_x": row(), "b_x": vec(),
        "w_y": row(), "b_y": vec(),
        "w_z": row(), "b_z": vec(),
        "w_bb": row(), "b_bb": vec(),
    }


def reference(act_dgram, aa_proj1, aa_proj2, esm_proj1, esm_proj2, query_embedding,
              pseudo_beta_mask, backbone_mask, multichain_mask_2d, unit_x, unit_y, unit_z,
              ln_g, ln_b, w_q, b_q, w_pbm, b_pbm, w_x, b_x, w_y, b_y, w_z, b_z, w_bb, b_bb):
    pbm, bbm, mc = f64(pseudo_beta_mask), f64(backbone_mask), f64(multichain_mask_2d)
    pb2 = pbm[:, None] * pbm[None, :] * mc
    bb2 = bbm[:, None] * bbm[None, :] * mc
    act = f64(act_dgram)
    act = act + (pb2[..., None] * f64(w_pbm)[0] + f64(b_pbm))
    act = act + f64(aa_proj1)[None, :, :]
    act = act + f64(aa_proj2)[:, None, :]
    act = act + ((f64(unit_x) * bb2)[..., None] * f64(w_x)[0] + f64(b_x))
    act = act + ((f64(unit_y) * bb2)[..., None] * f64(w_y)[0] + f64(b_y))
    act = act + ((f64(unit_z) * bb2)[..., None] * f64(w_z)[0] + f64(b_z))
    act = act + (bb2[..., None] * f64(w_bb)[0] + f64(b_bb))
    act = act + f64(esm_proj1)[None, :, :]
    act = act + f64(esm_proj2)[:, None, :]
    q = layer_norm(f64(query_embedding), f64(ln_g), f64(ln_b))
    act = act + (mxq(q, 2, "e4m3") @ mxq(f64(w_q), 0, "e4m3")) + f64(b_q)
    return act

@@ -1,0 +1,515 @@
+from contextlib import ExitStack
+
+import concourse.mybir as mybir
+from concourse.masks import make_identity
+
+F32 = mybir.dt.float32
+BF16 = mybir.dt.bfloat16
+U32 = mybir.dt.uint32
+U8 = mybir.dt.uint8
+FP8X4 = mybir.dt.float8_e4m3fn_x4
+ALU = mybir.AluOpType
+ACT = mybir.ActivationFunctionType
+
+P = 128
+N_RES = 64
+C_IN = 512
+C_OUT = 1024
+PACK = 4
+TILES = N_RES * N_RES // P
+BANK = 512
+BANKS = C_OUT // BANK
+LN_EPS = 1e-5
+
+PLAIN_COLS = 384
+VEC_COLS = C_OUT - PLAIN_COLS
+VEC_CHUNKS = VEC_COLS // P
+
+K_J = 0
+K_I = 64
+K_W = 96
+K_ONE = 101
+K_END = 107
+N_W = K_ONE - K_W
+I_HALF = N_RES // 2
+
+SUMMED_TERMS = 2
+CHAINED_TERMS = N_W - SUMMED_TERMS
+
+PLAIN_PIECES = 2
+PIECE_COLS = PLAIN_COLS // PLAIN_PIECES
+
+X_AHEAD = 7
+ACT_AHEAD = 2
+
+FLOPS = 2 * N_RES * N_RES * C_IN * C_OUT
+
+
+def tile_templatepairembeddermultimer_pa_t_kernel(
+    tc,
+    act_dgram,
+    aa_proj1,
+    aa_proj2,
+    esm_proj1,
+    esm_proj2,
+    query_embedding,
+    pseudo_beta_mask,
+    backbone_mask,
+    multichain_mask_2d,
+    unit_x,
+    unit_y,
+    unit_z,
+    ln_g,
+    ln_b,
+    w_q,
+    b_q,
+    w_pbm,
+    b_pbm,
+    w_x,
+    b_x,
+    w_y,
+    b_y,
+    w_z,
+    b_z,
+    w_bb,
+    b_bb,
+    out,
+):
+    nc = tc.nc
+    x_rows = query_embedding.flatten_outer_dims()
+    act_rows = act_dgram.flatten_outer_dims()
+    out_rows = out.flatten_outer_dims()
+    rank_one_rows = (w_x, w_y, w_z, w_bb, w_pbm)
+    bias_rows = (b_q, b_pbm, b_x, b_y, b_z, b_bb)
+
+    with ExitStack() as stack:
+        stack.enter_context(tc.manual_schedule())
+        const = stack.enter_context(tc.tile_pool(name="const", bufs=1))
+        setup = stack.enter_context(tc.tile_pool(name="setup", bufs=1))
+        x_pool = stack.enter_context(tc.tile_pool(name="x", bufs=X_AHEAD + 2))
+        act_pool = stack.enter_context(tc.tile_pool(name="act", bufs=ACT_AHEAD + 2))
+        stat_pool = stack.enter_context(tc.tile_pool(name="stat", bufs=6))
+        work = stack.enter_context(tc.tile_pool(name="work", bufs=2))
+        res_pool = stack.enter_context(tc.tile_pool(name="res", bufs=3))
+        psum_two = stack.enter_context(tc.psum_pool(name="psum_two", bufs=2))
+        psum_one = stack.enter_context(tc.psum_pool(name="psum_one", bufs=1))
+
+        x_tiles = {}
+        act_tiles = {}
+
+        def load_x(t):
+            x_tile = x_pool.tile([P, C_IN], BF16)
+            nc.sync.dma_start(out=x_tile[:], in_=x_rows[t * P : (t + 1) * P, :])
+            x_tiles[t] = x_tile
+
+        def load_act(t):
+            act_tile = act_pool.tile([P, C_OUT], BF16)
+            nc.sync.dma_start(out=act_tile[:], in_=act_rows[t * P : (t + 1) * P, :])
+            act_tiles[t] = act_tile
+
+        ident = const.tile([P, P], F32)
+        make_identity(nc, ident[:])
+        ident_bf = const.tile([P, P], BF16)
+        make_identity(nc, ident_bf[:])
+        neg_half = const.tile([P, 1], F32)
+        nc.vector.memset(neg_half[:], -0.5)
+
+        for t in range(X_AHEAD):
+            load_x(t)
+
+        vec_rows = setup.tile([P, P], BF16)
+        nc.vector.memset(vec_rows[:], 0.0)
+        gain_raw = setup.tile([P, PACK], BF16)
+        nc.sync.dma_start(out=gain_raw[:], in_=ln_g.rearrange("(p u) -> p u", u=PACK))
+        shift_raw = setup.tile([P, PACK], BF16)
+        nc.sync.dma_start(out=shift_raw[:], in_=ln_b.rearrange("(p u) -> p u", u=PACK))
+        residue_masks = (backbone_mask, pseudo_beta_mask)
+        for m in range(2):
+            nc.sync.dma_start(
+                out=vec_rows[m : m + 1, :].rearrange("o (h j) -> o h j", h=2),
+                in_=residue_masks[m].unsqueeze(0).unsqueeze(0).to_broadcast([1, 2, N_RES]),
+            )
+        pair_rows = setup.tile([P, P], BF16)
+        pair_inputs = (multichain_mask_2d, unit_x, unit_y, unit_z)
+        for x in range(4):
+            nc.sync.dma_start(
+                out=pair_rows[x * TILES : (x + 1) * TILES, :],
+                in_=pair_inputs[x].rearrange("(t h) j -> t (h j)", h=2),
+            )
+        mask_rows = setup.tile([P, 2, N_RES], BF16)
+        for m in range(2):
+            nc.sync.dma_start(out=mask_rows[:, m, :], in_=residue_masks[m].partition_broadcast(P))
+
+        table_a = setup.tile([P, 2, C_OUT], BF16)
+        table_e = setup.tile([P, 2, C_OUT], BF16)
+        nc.vector.memset(table_a[K_W:P, :, :], 0.0)
+        nc.vector.memset(table_e[K_W:P, :, :], 0.0)
+        nc.sync.dma_start(
+            out=table_a[K_J : K_J + N_RES, :, :], in_=aa_proj1.unsqueeze(1).to_broadcast([N_RES, 2, C_OUT])
+        )
+        nc.sync.dma_start(
+            out=table_e[K_J : K_J + N_RES, :, :], in_=esm_proj1.unsqueeze(1).to_broadcast([N_RES, 2, C_OUT])
+        )
+        nc.sync.dma_start(out=table_a[K_I : K_I + I_HALF, :, :], in_=aa_proj2.rearrange("(s m) c -> m s c", s=2))
+        nc.sync.dma_start(out=table_e[K_I : K_I + I_HALF, :, :], in_=esm_proj2.rearrange("(s m) c -> m s c", s=2))
+        for f in range(N_W):
+            nc.sync.dma_start(
+                out=table_a[K_W + f : K_W + f + 1, :, :],
+                in_=rank_one_rows[f].unsqueeze(1).to_broadcast([1, 2, C_OUT]),
+            )
+        for b in range(len(bias_rows)):
+            nc.sync.dma_start(
+                out=table_a[K_ONE + b : K_ONE + b + 1, :, :],
+                in_=bias_rows[b].unsqueeze(0).unsqueeze(0).to_broadcast([1, 2, C_OUT]),
+            )
+
+        w_raw = setup.tile([P, PACK, C_OUT], BF16)
+        nc.sync.dma_start(out=w_raw[:], in_=w_q.rearrange("(p u) c -> p u c", u=PACK))
+
+        w_all = const.tile([P, CHAINED_TERMS, VEC_COLS], BF16)
+        for f in range(CHAINED_TERMS):
+            nc.sync.dma_start(
+                out=w_all[:, f, :],
+                in_=rank_one_rows[f].rearrange("o c -> (o c)")[PLAIN_COLS:C_OUT].partition_broadcast(P),
+            )
+
+        for t in range(ACT_AHEAD):
+            load_act(t)
+
+        feat = const.tile([P, TILES, P], F32)
+        nc.vector.memset(feat[:, :, K_I:P], 0.0)
+        nc.vector.memset(feat[:, :, K_ONE:K_END], 1.0)
+        one_hot_j = setup.tile([P, N_RES], F32)
+        nc.vector.tensor_tensor(out=one_hot_j[:], in0=ident[:, 0:N_RES], in1=ident[:, N_RES:P], op=ALU.add)
+        nc.vector.tensor_copy(
+            out=feat[:, :, K_J : K_J + N_RES], in_=one_hot_j[:].unsqueeze(1).to_broadcast([P, TILES, N_RES])
+        )
+        feat_halves = feat[:].rearrange("p (s t) k -> p s (t k)", s=2)
+        diagonal_step = P + 2
+        for h in range(2):
+            first = K_I + h
+            nc.vector.memset(
+                feat_halves[h * N_RES : (h + 1) * N_RES, :, first : first + (TILES // 2 - 1) * diagonal_step + 1 : diagonal_step],
+                1.0,
+            )
+
+        vec_cols_ps = psum_two.tile([P, P], BF16, tag="extra")
+        nc.tensor.transpose(vec_cols_ps[:], vec_rows[:], ident_bf[:])
+        pair_cols_ps = psum_two.tile([P, P], BF16, tag="extra")
+        nc.tensor.transpose(pair_cols_ps[:], pair_rows[:], ident_bf[:])
+        vec_cols = const.tile([P, 2 * PACK + 2], F32)
+        nc.vector.tensor_copy(out=vec_cols[:, 0:PACK], in_=gain_raw[:])
+        nc.vector.tensor_copy(out=vec_cols[:, PACK : 2 * PACK], in_=shift_raw[:])
+        nc.vector.tensor_copy(out=vec_cols[:, 2 * PACK : 2 * PACK + 2], in_=vec_cols_ps[:, 0:2])
+
+        pair_mask = setup.tile([P, 2, TILES], F32)
+        for h in range(2):
+            half = slice(h * N_RES, (h + 1) * N_RES)
+            for m in range(2):
+                nc.vector.tensor_scalar(
+                    out=pair_mask[half, m, :],
+                    in0=mask_rows[half, m, h:N_RES:2],
+                    scalar1=vec_cols[half, 2 * PACK + m : 2 * PACK + m + 1],
+                    scalar2=None,
+                    op0=ALU.mult,
+                )
+        nc.vector.tensor_tensor(
+            out=pair_mask[:],
+            in0=pair_mask[:],
+            in1=pair_cols_ps[:, 0:TILES].unsqueeze(1).to_broadcast([P, 2, TILES]),
+            op=ALU.mult,
+        )
+        nc.vector.tensor_tensor(
+            out=feat[:, :, K_W : K_W + 3].rearrange("p t x -> p x t"),
+            in0=pair_cols_ps[:, TILES:P].rearrange("p (x t) -> p x t", x=3),
+            in1=pair_mask[:, 0:1, :].to_broadcast([P, 3, TILES]),
+            op=ALU.mult,
+        )
+        nc.vector.tensor_copy(out=feat[:, :, K_W + 3 : K_W + 5].rearrange("p t m -> p m t"), in_=pair_mask[:])
+
+        table = const.tile([P, 2, C_OUT], F32)
+        nc.vector.tensor_tensor(out=table[:], in0=table_a[:], in1=table_e[:], op=ALU.add)
+
+        a_twice = const.tile([P, VEC_CHUNKS, 2, N_RES], F32)
+        b_cols = const.tile([P, VEC_CHUNKS, N_RES], F32)
+        w_cols = const.tile([P, VEC_CHUNKS, N_W], F32)
+        for c in range(VEC_CHUNKS):
+            chunk = slice(PLAIN_COLS + c * P, PLAIN_COLS + (c + 1) * P)
+            table_t = psum_two.tile([P, 2, P], F32, tag="extra")
+            for s in range(2):
+                nc.tensor.transpose(table_t[:, s, :], table[:, s, chunk], ident[:])
+            nc.vector.tensor_copy(
+                out=a_twice[:, c, :, :],
+                in_=table_t[:, 0, K_J : K_J + N_RES].unsqueeze(1).to_broadcast([P, 2, N_RES]),
+            )
+            nc.vector.tensor_copy(out=w_cols[:, c, :], in_=table_t[:, 0, K_W : K_W + N_W])
+            bias_sum = stat_pool.tile([P, 1], F32)
+            nc.vector.reduce_sum(out=bias_sum[:], in_=table_t[:, 0, K_ONE:K_END], axis=mybir.AxisListType.X)
+            nc.vector.tensor_scalar(
+                out=b_cols[:, c, :].rearrange("p (s m) -> p s m", s=2),
+                in0=table_t[:, :, K_I : K_I + I_HALF],
+                scalar1=bias_sum[:, 0:1],
+                scalar2=None,
+                op0=ALU.add,
+            )
+
+        w_grouped = setup.tile([P, C_OUT, PACK], BF16, align_bytes=64)
+        nc.vector.tensor_copy(
+            out=w_grouped[:].rearrange("p (c i) u -> p c u i", i=4),
+            in_=w_raw[:].rearrange("p u (c i) -> p c u i", i=4),
+        )
+        w_codes = const.tile([P, C_OUT], U32, align_bytes=64)
+        w_scales = const.tile([P, C_OUT], U8, align_bytes=64)
+        nc.vector.quantize_mx(
+            out=w_codes[:].bitcast(FP8X4), scales=w_scales[:], in_=w_grouped[:].rearrange("p c u -> p (c u)")
+        )
+
+        moments = {}
+        x_hats = {}
+        x_hat_ts = {}
+        q_planes = {}
+        q_groupeds = {}
+        q_words = {}
+        products = {}
+        sides = {}
+        feat_ts = {}
+        summands = {}
+        extras = {}
+        results = {}
+        partials = {}
+
+        def ln_sum(t):
+            unread_sum = work.tile([P, C_IN], BF16)
+            row_sum = stat_pool.tile([P, 1], F32)
+            nc.scalar.activation(out=unread_sum[:], in_=x_tiles[t][:], func=ACT.Identity, accum_out=row_sum[:])
+            moment = stat_pool.tile([P, 4], F32)
+            nc.gpsimd.tensor_scalar(
+                out=moment[:, 0:1], in0=row_sum[:], scalar1=-1.0 / C_IN, scalar2=0.0, op0=ALU.mult, op1=ALU.add
+            )
+            moments[t] = moment
+
+        def ln_var(t):
+            moment = moments[t]
+            unread_sq = work.tile([P, C_IN], BF16)
+            sq_sum = stat_pool.tile([P, 1], F32)
+            nc.scalar.activation(
+                out=unread_sq[:], in_=x_tiles[t][:], func=ACT.Square, bias=moment[:, 0:1], accum_out=sq_sum[:]
+            )
+            nc.gpsimd.tensor_scalar(
+                out=moment[:, 1:2], in0=sq_sum[:], scalar1=1.0 / C_IN, scalar2=LN_EPS, op0=ALU.mult, op1=ALU.add
+            )
+            nc.gpsimd.tensor_tensor(out=moment[:, 2:3], in0=moment[:, 1:2], in1=neg_half[:], op=ALU.pow)
+            nc.gpsimd.tensor_tensor(out=moment[:, 3:4], in0=moment[:, 0:1], in1=moment[:, 2:3], op=ALU.mult)
+
+        def ln_norm(t):
+            moment = moments[t]
+            x_hat = work.tile([P, PACK, P], F32)
+            nc.scalar.activation(
+                out=x_hat[:], in_=x_tiles[t][:].rearrange("r (p u) -> r u p", u=PACK), func=ACT.Identity, scale=moment[:, 2:3], bias=moment[:, 3:4]
+            )
+            x_hats[t] = x_hat
+
+        def ln_transpose(t):
+            x_hat_t = psum_one.tile([P, PACK, P], F32)
+            for u in range(PACK):
+                nc.tensor.transpose(x_hat_t[:, u, :], x_hats[t][:, u, :], ident[:])
+            x_hat_ts[t] = x_hat_t
+
+        def ln_affine(t):
+            q_plane = work.tile([P, PACK, P], BF16)
+            for u in range(PACK):
+                nc.scalar.activation(
+                    out=q_plane[:, u, :],
+                    in_=x_hat_ts[t][:, u, :],
+                    func=ACT.Identity,
+                    scale=vec_cols[:, u : u + 1],
+                    bias=vec_cols[:, PACK + u : PACK + u + 1],
+                )
+            q_planes[t] = q_plane
+
+        def regroup(t):
+            q_grouped = work.tile([P, P, PACK], BF16, align_bytes=64)
+            nc.vector.tensor_copy(
+                out=q_grouped[:].rearrange("p (r i) u -> p r u i", i=4),
+                in_=q_planes[t][:].rearrange("p u (r i) -> p r u i", i=4),
+            )
+            q_groupeds[t] = q_grouped
+
+        def quantise(t):
+            q_codes = work.tile([P, P], U32, align_bytes=64)
+            q_scales = work.tile([P, P], U8, align_bytes=64)
+            nc.vector.quantize_mx(
+                out=q_codes[:].bitcast(FP8X4),
+                scales=q_scales[:],
+                in_=q_groupeds[t][:].rearrange("p r u -> p (r u)"),
+            )
+            q_words[t] = (q_codes, q_scales)
+
+        def project(t):
+            q_codes, q_scales = q_words[t]
+            product = psum_one.tile([P, C_OUT], F32)
+            for bank in range(BANKS):
+                cols = slice(bank * BANK, (bank + 1) * BANK)
+                nc.tensor.matmul_mx(
+                    out=product[:, cols],
+                    lhsT=q_codes[:].bitcast(FP8X4),
+                    lhsT_scale=q_scales[:],
+                    rhs=w_codes[:, cols].bitcast(FP8X4),
+                    rhs_scale=w_scales[:, cols],
+                    start=True,
+                    stop=True,
+                )
+            products[t] = product
+
+        def feat_transpose(t):
+            side = psum_one.tile([P, 1 + SUMMED_TERMS, P], F32)
+            nc.tensor.transpose(side[:, 0, :], feat[:, t, :], ident[:])
+            for s in range(SUMMED_TERMS):
+                k = K_W + CHAINED_TERMS + s
+                nc.tensor.transpose(side[:, 1 + s, :], feat[:, t, k : k + 1].to_broadcast([P, P]), ident[:])
+            sides[t] = side
+
+        def feat_copy(t):
+            feat_t = work.tile([P, P], F32)
+            nc.scalar.copy(out=feat_t[:], in_=sides[t][:, 0, :])
+            feat_ts[t] = feat_t
+
+        def multiply(t):
+            summand = work.tile([P, SUMMED_TERMS, VEC_CHUNKS, P], F32)
+            for c in range(VEC_CHUNKS):
+                for h in range(2):
+                    i = 2 * t + h
+                    nc.scalar.activation(
+                        out=summand[:, 0, c, h * N_RES : (h + 1) * N_RES],
+                        in_=sides[t][:, 1, h * N_RES : (h + 1) * N_RES],
+                        func=ACT.Identity,
+                        scale=w_cols[:, c, CHAINED_TERMS : CHAINED_TERMS + 1],
+                        bias=b_cols[:, c, i : i + 1],
+                    )
+                for s in range(1, SUMMED_TERMS):
+                    nc.scalar.activation(
+                        out=summand[:, s, c, :],
+                        in_=sides[t][:, 1 + s, :],
+                        func=ACT.Identity,
+                        scale=w_cols[:, c, CHAINED_TERMS + s : CHAINED_TERMS + s + 1],
+                    )
+            summands[t] = summand
+
+        def sum_chunks(t, chunks):
+            for c in chunks:
+                chunk = slice(PLAIN_COLS + c * P, PLAIN_COLS + (c + 1) * P)
+                nc.tensor.matmul(
+                    out=extras[t][:, chunk],
+                    lhsT=a_twice[:, c, :, :].rearrange("p h j -> p (h j)"),
+                    rhs=ident[:],
+                    is_transpose=True,
+                    start=True,
+                    stop=False,
+                )
+                for s in range(SUMMED_TERMS):
+                    nc.tensor.matmul(
+                        out=extras[t][:, chunk],
+                        lhsT=summands[t][:, s, c, :],
+                        rhs=ident[:],
+                        is_transpose=True,
+                        start=False,
+                        stop=(s == SUMMED_TERMS - 1),
+                    )
+
+        def plain_piece(t, piece):
+            cols = slice(piece * PIECE_COLS, (piece + 1) * PIECE_COLS)
+            nc.tensor.matmul(
+                out=extras[t][:, cols],
+                lhsT=feat_ts[t][:],
+                rhs=table[:, t // (TILES // 2), cols],
+                start=True,
+                stop=True,
+            )
+
+        def small_terms_first(t):
+            extra = psum_two.tile([P, C_OUT], F32)
+            extras[t] = extra
+            sum_chunks(t, (4, 3))
+            plain_piece(t, 0)
+
+        def small_terms_second(t):
+            sum_chunks(t, (2,))
+
+        def small_terms_third(t):
+            sum_chunks(t, (1, 0))
+            plain_piece(t, 1)
+
+        def combine_open(t):
+            result = res_pool.tile([P, C_OUT], F32)
+            partial = work.tile([P, VEC_COLS], F32)
+            first, second = slice(0, BANK), slice(BANK, C_OUT)
+            nc.vector.scalar_tensor_tensor(
+                out=partial[:, BANK - PLAIN_COLS : VEC_COLS],
+                in0=w_all[:, 0, BANK - PLAIN_COLS : VEC_COLS],
+                scalar=feat[:, t, K_W : K_W + 1],
+                in1=products[t][:, second],
+                op0=ALU.mult,
+                op1=ALU.add,
+            )
+            nc.vector.tensor_tensor(out=result[:, first], in0=act_tiles[t][:, first], in1=products[t][:, first], op=ALU.add)
+            nc.vector.tensor_tensor(out=result[:, second], in0=act_tiles[t][:, second], in1=extras[t][:, second], op=ALU.add)
+            nc.vector.scalar_tensor_tensor(
+                out=partial[:, 0 : BANK - PLAIN_COLS],
+                in0=w_all[:, 0, 0 : BANK - PLAIN_COLS],
+                scalar=feat[:, t, K_W : K_W + 1],
+                in1=extras[t][:, PLAIN_COLS:BANK],
+                op0=ALU.mult,
+                op1=ALU.add,
+            )
+            nc.vector.tensor_tensor(
+                out=result[:, 0:PLAIN_COLS], in0=result[:, 0:PLAIN_COLS], in1=extras[t][:, 0:PLAIN_COLS], op=ALU.add
+            )
+            results[t] = result
+            partials[t] = partial
+
+        def combine_rank_one(t):
+            for f in range(1, CHAINED_TERMS):
+                running = results[t][:, PLAIN_COLS:C_OUT] if f % 2 == 1 else partials[t][:]
+                nc.vector.scalar_tensor_tensor(
+                    out=running,
+                    in0=w_all[:, f, :],
+                    scalar=feat[:, t, K_W + f : K_W + f + 1],
+                    in1=running,
+                    op0=ALU.mult,
+                    op1=ALU.add,
+                )
+
+        def combine_close(t):
+            nc.gpsimd.tensor_tensor(
+                out=results[t][:, PLAIN_COLS:C_OUT], in0=results[t][:, PLAIN_COLS:C_OUT], in1=partials[t][:], op=ALU.add
+            )
+
+        def store(t):
+            nc.sync.dma_start(out=out_rows[t * P : (t + 1) * P, :], in_=results[t][:])
+
+        def each(stage, t):
+            if 0 <= t < TILES:
+                stage(t)
+
+        for n in range(-6, TILES + 1):
+            if n >= 0:
+                each(load_x, n + X_AHEAD)
+                each(load_act, n + ACT_AHEAD)
+            each(combine_close, n - 1)
+            each(store, n - 1)
+            each(ln_affine, n + 2)
+            each(feat_copy, n + 2)
+            each(multiply, n + 2)
+            each(ln_norm, n + 4)
+            each(ln_var, n + 5)
+            each(ln_sum, n + 6)
+            each(combine_open, n)
+            each(small_terms_first, n + 1)
+            each(ln_transpose, n + 3)
+            each(small_terms_second, n + 1)
+            each(project, n + 1)
+            each(small_terms_third, n + 1)
+            each(feat_transpose, n + 3)
+            each(regroup, n + 2)
+            each(combine_rank_one, n)
+            each(quantise, n + 2)

@@ -13,10 +13,11 @@ ACT = mybir.ActivationFunctionType
 
 P = 128
 N_RES = 64
+PAIRS = N_RES * N_RES
 C_IN = 512
 C_OUT = 1024
 PACK = 4
-TILES = N_RES * N_RES // P
+TILES = PAIRS // P
 BANK = 512
 BANKS = C_OUT // BANK
 LN_EPS = 1e-5
@@ -32,15 +33,22 @@ K_ONE = 101
 K_END = 107
 N_W = K_ONE - K_W
 I_HALF = N_RES // 2
+HALF_TILES = TILES // 2
+HALF_PAIRS = PAIRS // 2
 
-SUMMED_TERMS = 2
-CHAINED_TERMS = N_W - SUMMED_TERMS
+OPEN_TERM, CHAIN_TERM, POOL_TERM, BIASED_TERM, SCALAR_TERM = range(N_W)
+SPREAD_FIRST = POOL_TERM
+N_SPREAD = N_W - SPREAD_FIRST
+
+GROUP = 512
+GROUP_TILES = GROUP // P
+PAIR_COLS = 2 * P
 
 PLAIN_PIECES = 2
 PIECE_COLS = PLAIN_COLS // PLAIN_PIECES
 
-X_AHEAD = 7
-ACT_AHEAD = 2
+X_AHEAD = 8
+ACT_AHEAD = 3
 
 FLOPS = 2 * N_RES * N_RES * C_IN * C_OUT
 
@@ -81,21 +89,26 @@ def tile_templatepairembeddermultimer_pa_t_kernel(
     out_rows = out.flatten_outer_dims()
     rank_one_rows = (w_x, w_y, w_z, w_bb, w_pbm)
     bias_rows = (b_q, b_pbm, b_x, b_y, b_z, b_bb)
+    scratch = out.rearrange("i j c -> (i j c)")[PAIRS * C_OUT - N_W * PAIRS : PAIRS * C_OUT].rearrange(
+        "(s n) -> s n", n=PAIRS
+    )
 
     with ExitStack() as stack:
         stack.enter_context(tc.manual_schedule())
         const = stack.enter_context(tc.tile_pool(name="const", bufs=1))
         setup = stack.enter_context(tc.tile_pool(name="setup", bufs=1))
-        x_pool = stack.enter_context(tc.tile_pool(name="x", bufs=X_AHEAD + 2))
+        x_pool = stack.enter_context(tc.tile_pool(name="x", bufs=X_AHEAD))
         act_pool = stack.enter_context(tc.tile_pool(name="act", bufs=ACT_AHEAD + 2))
-        stat_pool = stack.enter_context(tc.tile_pool(name="stat", bufs=6))
-        work = stack.enter_context(tc.tile_pool(name="work", bufs=2))
-        res_pool = stack.enter_context(tc.tile_pool(name="res", bufs=3))
+        stat_pool = stack.enter_context(tc.tile_pool(name="stat", bufs=8))
+        spread_pool = stack.enter_context(tc.tile_pool(name="spread", bufs=3))
+        work = stack.enter_context(tc.tile_pool(name="work", bufs=3))
+        res_pool = stack.enter_context(tc.tile_pool(name="res", bufs=4))
         psum_two = stack.enter_context(tc.psum_pool(name="psum_two", bufs=2))
         psum_one = stack.enter_context(tc.psum_pool(name="psum_one", bufs=1))
 
         x_tiles = {}
         act_tiles = {}
+        spread_tiles = {}
 
         def load_x(t):
             x_tile = x_pool.tile([P, C_IN], BF16)
@@ -107,205 +120,202 @@ def tile_templatepairembeddermultimer_pa_t_kernel(
             nc.sync.dma_start(out=act_tile[:], in_=act_rows[t * P : (t + 1) * P, :])
             act_tiles[t] = act_tile
 
-        ident = const.tile([P, P], F32)
-        make_identity(nc, ident[:])
-        ident_bf = const.tile([P, P], BF16)
-        make_identity(nc, ident_bf[:])
-        neg_half = const.tile([P, 1], F32)
-        nc.vector.memset(neg_half[:], -0.5)
+        def load_spread(g):
+            spread = spread_pool.tile([P, N_SPREAD, GROUP], F32)
+            nc.sync.dma_start(
+                out=spread[:],
+                in_=scratch[SPREAD_FIRST:N_W, g * GROUP : (g + 1) * GROUP].partition_broadcast(P),
+            )
+            spread_tiles[g] = spread
 
-        for t in range(X_AHEAD):
-            load_x(t)
-
+        load_x(0)
         vec_rows = setup.tile([P, P], BF16)
         nc.vector.memset(vec_rows[:], 0.0)
-        gain_raw = setup.tile([P, PACK], BF16)
-        nc.sync.dma_start(out=gain_raw[:], in_=ln_g.rearrange("(p u) -> p u", u=PACK))
-        shift_raw = setup.tile([P, PACK], BF16)
-        nc.sync.dma_start(out=shift_raw[:], in_=ln_b.rearrange("(p u) -> p u", u=PACK))
         residue_masks = (backbone_mask, pseudo_beta_mask)
         for m in range(2):
             nc.sync.dma_start(
                 out=vec_rows[m : m + 1, :].rearrange("o (h j) -> o h j", h=2),
                 in_=residue_masks[m].unsqueeze(0).unsqueeze(0).to_broadcast([1, 2, N_RES]),
             )
-        pair_rows = setup.tile([P, P], BF16)
-        pair_inputs = (multichain_mask_2d, unit_x, unit_y, unit_z)
-        for x in range(4):
-            nc.sync.dma_start(
-                out=pair_rows[x * TILES : (x + 1) * TILES, :],
-                in_=pair_inputs[x].rearrange("(t h) j -> t (h j)", h=2),
-            )
         mask_rows = setup.tile([P, 2, N_RES], BF16)
         for m in range(2):
             nc.sync.dma_start(out=mask_rows[:, m, :], in_=residue_masks[m].partition_broadcast(P))
-
-        table_a = setup.tile([P, 2, C_OUT], BF16)
-        table_e = setup.tile([P, 2, C_OUT], BF16)
-        nc.vector.memset(table_a[K_W:P, :, :], 0.0)
-        nc.vector.memset(table_e[K_W:P, :, :], 0.0)
-        nc.sync.dma_start(
-            out=table_a[K_J : K_J + N_RES, :, :], in_=aa_proj1.unsqueeze(1).to_broadcast([N_RES, 2, C_OUT])
-        )
-        nc.sync.dma_start(
-            out=table_e[K_J : K_J + N_RES, :, :], in_=esm_proj1.unsqueeze(1).to_broadcast([N_RES, 2, C_OUT])
-        )
-        nc.sync.dma_start(out=table_a[K_I : K_I + I_HALF, :, :], in_=aa_proj2.rearrange("(s m) c -> m s c", s=2))
-        nc.sync.dma_start(out=table_e[K_I : K_I + I_HALF, :, :], in_=esm_proj2.rearrange("(s m) c -> m s c", s=2))
-        for f in range(N_W):
-            nc.sync.dma_start(
-                out=table_a[K_W + f : K_W + f + 1, :, :],
-                in_=rank_one_rows[f].unsqueeze(1).to_broadcast([1, 2, C_OUT]),
-            )
-        for b in range(len(bias_rows)):
-            nc.sync.dma_start(
-                out=table_a[K_ONE + b : K_ONE + b + 1, :, :],
-                in_=bias_rows[b].unsqueeze(0).unsqueeze(0).to_broadcast([1, 2, C_OUT]),
-            )
-
+        multichain = setup.tile([P, N_RES], BF16)
+        units = setup.tile([P, 2, N_RES], BF16)
+        for b in range(2):
+            nc.sync.dma_start(out=multichain[b * N_RES : (b + 1) * N_RES, :], in_=multichain_mask_2d[:, :])
+        nc.sync.dma_start(out=units[0:N_RES, 0, :], in_=unit_x[:, :])
+        nc.sync.dma_start(out=units[N_RES:P, 0, :], in_=unit_y[:, :])
+        nc.sync.dma_start(out=units[0:N_RES, 1, :], in_=unit_z[:, :])
+        nc.vector.memset(units[N_RES:P, 1, :], 1.0)
+        load_x(1)
         w_raw = setup.tile([P, PACK, C_OUT], BF16)
-        nc.sync.dma_start(out=w_raw[:], in_=w_q.rearrange("(p u) c -> p u c", u=PACK))
+        for b in range(BANKS):
+            cols = slice(b * BANK, (b + 1) * BANK)
+            nc.sync.dma_start(out=w_raw[:, :, cols], in_=w_q.rearrange("(p u) c -> p u c", u=PACK)[:, :, cols])
+        gain_raw = setup.tile([P, PACK], BF16)
+        nc.sync.dma_start(out=gain_raw[:], in_=ln_g.rearrange("(p u) -> p u", u=PACK))
+        shift_raw = setup.tile([P, PACK], BF16)
+        nc.sync.dma_start(out=shift_raw[:], in_=ln_b.rearrange("(p u) -> p u", u=PACK))
+        load_x(2)
 
-        w_all = const.tile([P, CHAINED_TERMS, VEC_COLS], BF16)
-        for f in range(CHAINED_TERMS):
+        cols_a = setup.tile([P, VEC_COLS], BF16)
+        cols_e = setup.tile([P, VEC_COLS], BF16)
+        nc.sync.dma_start(out=cols_a[0:N_RES, :], in_=aa_proj1[:, PLAIN_COLS:C_OUT])
+        nc.sync.dma_start(out=cols_a[N_RES:P, :], in_=aa_proj2[:, PLAIN_COLS:C_OUT])
+        nc.sync.dma_start(out=cols_e[0:N_RES, :], in_=esm_proj1[:, PLAIN_COLS:C_OUT])
+        nc.sync.dma_start(out=cols_e[N_RES:P, :], in_=esm_proj2[:, PLAIN_COLS:C_OUT])
+        small_rows = setup.tile([P, C_OUT], BF16)
+        nc.vector.memset(small_rows[:], 0.0)
+        for r, row in enumerate(rank_one_rows):
+            nc.sync.dma_start(out=small_rows[K_W + r : K_W + r + 1, :], in_=row[:, :])
+        for r, row in enumerate(bias_rows):
+            nc.sync.dma_start(out=small_rows[K_ONE + r : K_ONE + r + 1, :], in_=row.unsqueeze(0))
+        table_a = setup.tile([K_W, 2, PLAIN_COLS], BF16)
+        table_e = setup.tile([K_W, 2, PLAIN_COLS], BF16)
+        for tab, by_j, by_i in ((table_a, aa_proj1, aa_proj2), (table_e, esm_proj1, esm_proj2)):
             nc.sync.dma_start(
-                out=w_all[:, f, :],
-                in_=rank_one_rows[f].rearrange("o c -> (o c)")[PLAIN_COLS:C_OUT].partition_broadcast(P),
+                out=tab[K_J : K_J + N_RES, :, :],
+                in_=by_j[:, 0:PLAIN_COLS].unsqueeze(1).to_broadcast([N_RES, 2, PLAIN_COLS]),
+            )
+            nc.sync.dma_start(
+                out=tab[K_I : K_I + I_HALF, :, :], in_=by_i.rearrange("(s m) c -> m s c", s=2)[:, :, 0:PLAIN_COLS]
             )
 
-        for t in range(ACT_AHEAD):
-            load_act(t)
+        ident = const.tile([P, P], F32)
+        make_identity(nc, ident[:])
+        ident_bf = const.tile([P, P], BF16)
+        make_identity(nc, ident_bf[:])
 
-        feat = const.tile([P, TILES, P], F32)
-        nc.vector.memset(feat[:, :, K_I:P], 0.0)
-        nc.vector.memset(feat[:, :, K_ONE:K_END], 1.0)
-        one_hot_j = setup.tile([P, N_RES], F32)
-        nc.vector.tensor_tensor(out=one_hot_j[:], in0=ident[:, 0:N_RES], in1=ident[:, N_RES:P], op=ALU.add)
-        nc.vector.tensor_copy(
-            out=feat[:, :, K_J : K_J + N_RES], in_=one_hot_j[:].unsqueeze(1).to_broadcast([P, TILES, N_RES])
+        feat_t = const.tile([P, HALF_PAIRS], F32)
+        nc.vector.memset(feat_t[K_W:P, :], 1.0)
+        nc.scalar.copy(
+            out=feat_t[K_J : K_J + N_RES, :].rearrange("k (i j) -> k i j", j=N_RES),
+            in_=ident[0:N_RES, 0:N_RES].unsqueeze(1).to_broadcast([N_RES, I_HALF, N_RES]),
         )
-        feat_halves = feat[:].rearrange("p (s t) k -> p s (t k)", s=2)
-        diagonal_step = P + 2
-        for h in range(2):
-            first = K_I + h
-            nc.vector.memset(
-                feat_halves[h * N_RES : (h + 1) * N_RES, :, first : first + (TILES // 2 - 1) * diagonal_step + 1 : diagonal_step],
-                1.0,
+        for q in range(4):
+            i_cols = slice(K_I + q * 8, K_I + (q + 1) * 8)
+            nc.gpsimd.tensor_scalar(
+                out=feat_t[K_I : K_I + I_HALF, q * GROUP : (q + 1) * GROUP].rearrange("k (i j) -> k i j", j=N_RES),
+                in0=ident[K_I : K_I + I_HALF, i_cols].unsqueeze(2).to_broadcast([I_HALF, 8, N_RES]),
+                scalar1=1.0,
+                scalar2=0.0,
+                op0=ALU.mult,
+                op1=ALU.add,
             )
 
         vec_cols_ps = psum_two.tile([P, P], BF16, tag="extra")
         nc.tensor.transpose(vec_cols_ps[:], vec_rows[:], ident_bf[:])
-        pair_cols_ps = psum_two.tile([P, P], BF16, tag="extra")
-        nc.tensor.transpose(pair_cols_ps[:], pair_rows[:], ident_bf[:])
-        vec_cols = const.tile([P, 2 * PACK + 2], F32)
+        mask_cols = const.tile([P, 2], F32)
+        nc.vector.tensor_copy(out=mask_cols[:], in_=vec_cols_ps[:, 0:2])
+        pair_masks = setup.tile([P, 2, N_RES], F32)
+        for m in range(2):
+            nc.vector.scalar_tensor_tensor(
+                out=pair_masks[:, m, :],
+                in0=multichain[:],
+                scalar=mask_cols[:, m : m + 1],
+                in1=mask_rows[:, m, :],
+                op0=ALU.mult,
+                op1=ALU.mult,
+            )
+        weights = setup.tile([P, 2, N_RES], F32)
+        nc.vector.tensor_tensor(
+            out=weights[:], in0=units[:], in1=pair_masks[:, 0:1, :].to_broadcast([P, 2, N_RES]), op=ALU.mult
+        )
+        for g in range(2):
+            nc.sync.dma_start(
+                out=scratch[2 * g : 2 * g + 2, :].rearrange("b (i j) -> (b i) j", j=N_RES), in_=weights[:, g, :]
+            )
+        nc.sync.dma_start(
+            out=scratch[N_W - 1 : N_W, :].rearrange("b (i j) -> (b i) j", j=N_RES), in_=pair_masks[0:N_RES, 1, :]
+        )
+        load_spread(0)
+        weight_rows = setup.tile([P, P], F32)
+        nc.sync.dma_start(
+            out=weight_rows[:], in_=scratch[0 : P // TILES, :].rearrange("s (t p) -> (s t) p", p=P)
+        )
+
+        def load_features(first_tile, tiles):
+            first = first_tile * P
+            nc.sync.dma_start(
+                out=feat_t[K_W:K_ONE, first % HALF_PAIRS : first % HALF_PAIRS + tiles * P],
+                in_=scratch[:, first : first + tiles * P],
+            )
+
+        load_features(0, HALF_TILES)
+        load_x(3)
+        load_x(4)
+        load_act(0)
+        load_act(1)
+        load_spread(1)
+        load_x(5)
+        load_act(2)
+        load_x(6)
+
+        vec_cols = const.tile([P, 2 * PACK], F32)
         nc.vector.tensor_copy(out=vec_cols[:, 0:PACK], in_=gain_raw[:])
         nc.vector.tensor_copy(out=vec_cols[:, PACK : 2 * PACK], in_=shift_raw[:])
-        nc.vector.tensor_copy(out=vec_cols[:, 2 * PACK : 2 * PACK + 2], in_=vec_cols_ps[:, 0:2])
 
-        pair_mask = setup.tile([P, 2, TILES], F32)
-        for h in range(2):
-            half = slice(h * N_RES, (h + 1) * N_RES)
-            for m in range(2):
-                nc.vector.tensor_scalar(
-                    out=pair_mask[half, m, :],
-                    in0=mask_rows[half, m, h:N_RES:2],
-                    scalar1=vec_cols[half, 2 * PACK + m : 2 * PACK + m + 1],
-                    scalar2=None,
-                    op0=ALU.mult,
-                )
-        nc.vector.tensor_tensor(
-            out=pair_mask[:],
-            in0=pair_mask[:],
-            in1=pair_cols_ps[:, 0:TILES].unsqueeze(1).to_broadcast([P, 2, TILES]),
-            op=ALU.mult,
-        )
-        nc.vector.tensor_tensor(
-            out=feat[:, :, K_W : K_W + 3].rearrange("p t x -> p x t"),
-            in0=pair_cols_ps[:, TILES:P].rearrange("p (x t) -> p x t", x=3),
-            in1=pair_mask[:, 0:1, :].to_broadcast([P, 3, TILES]),
-            op=ALU.mult,
-        )
-        nc.vector.tensor_copy(out=feat[:, :, K_W + 3 : K_W + 5].rearrange("p t m -> p m t"), in_=pair_mask[:])
-
-        table = const.tile([P, 2, C_OUT], F32)
-        nc.vector.tensor_tensor(out=table[:], in0=table_a[:], in1=table_e[:], op=ALU.add)
-
-        a_twice = const.tile([P, VEC_CHUNKS, 2, N_RES], F32)
-        b_cols = const.tile([P, VEC_CHUNKS, N_RES], F32)
-        w_cols = const.tile([P, VEC_CHUNKS, N_W], F32)
-        for c in range(VEC_CHUNKS):
-            chunk = slice(PLAIN_COLS + c * P, PLAIN_COLS + (c + 1) * P)
-            table_t = psum_two.tile([P, 2, P], F32, tag="extra")
-            for s in range(2):
-                nc.tensor.transpose(table_t[:, s, :], table[:, s, chunk], ident[:])
-            nc.vector.tensor_copy(
-                out=a_twice[:, c, :, :],
-                in_=table_t[:, 0, K_J : K_J + N_RES].unsqueeze(1).to_broadcast([P, 2, N_RES]),
-            )
-            nc.vector.tensor_copy(out=w_cols[:, c, :], in_=table_t[:, 0, K_W : K_W + N_W])
-            bias_sum = stat_pool.tile([P, 1], F32)
-            nc.vector.reduce_sum(out=bias_sum[:], in_=table_t[:, 0, K_ONE:K_END], axis=mybir.AxisListType.X)
-            nc.vector.tensor_scalar(
-                out=b_cols[:, c, :].rearrange("p (s m) -> p s m", s=2),
-                in0=table_t[:, :, K_I : K_I + I_HALF],
-                scalar1=bias_sum[:, 0:1],
-                scalar2=None,
-                op0=ALU.add,
-            )
-
-        w_grouped = setup.tile([P, C_OUT, PACK], BF16, align_bytes=64)
-        nc.vector.tensor_copy(
-            out=w_grouped[:].rearrange("p (c i) u -> p c u i", i=4),
-            in_=w_raw[:].rearrange("p u (c i) -> p c u i", i=4),
-        )
-        w_codes = const.tile([P, C_OUT], U32, align_bytes=64)
-        w_scales = const.tile([P, C_OUT], U8, align_bytes=64)
-        nc.vector.quantize_mx(
-            out=w_codes[:].bitcast(FP8X4), scales=w_scales[:], in_=w_grouped[:].rearrange("p c u -> p (c u)")
-        )
-
-        moments = {}
+        stats = {}
         x_hats = {}
         x_hat_ts = {}
         q_planes = {}
         q_groupeds = {}
         q_words = {}
         products = {}
-        sides = {}
-        feat_ts = {}
-        summands = {}
+        pool_sums = {}
+        biased_sums = {}
+        scalar_sums = {}
         extras = {}
         results = {}
         partials = {}
 
+        w_codes = const.tile([P, C_OUT], U32, align_bytes=64)
+        w_scales = const.tile([P, C_OUT], U8, align_bytes=64)
+        a_twice = const.tile([P, VEC_CHUNKS, 2, N_RES], F32)
+        b_cols = const.tile([P, VEC_CHUNKS, N_RES], F32)
+        w_cols = const.tile([P, VEC_CHUNKS, N_W], F32)
+        open_row = const.tile([P, VEC_COLS], BF16)
+        weight_cols = const.tile([P, P], F32)
+        table = const.tile([P, 2, PLAIN_COLS], F32)
+        chain_row = psum_one.tile([P, VEC_COLS], BF16)
+
         def ln_sum(t):
             unread_sum = work.tile([P, C_IN], BF16)
-            row_sum = stat_pool.tile([P, 1], F32)
-            nc.scalar.activation(out=unread_sum[:], in_=x_tiles[t][:], func=ACT.Identity, accum_out=row_sum[:])
-            moment = stat_pool.tile([P, 4], F32)
-            nc.gpsimd.tensor_scalar(
-                out=moment[:, 0:1], in0=row_sum[:], scalar1=-1.0 / C_IN, scalar2=0.0, op0=ALU.mult, op1=ALU.add
+            stat = stat_pool.tile([P, 4], F32)
+            nc.scalar.activation(
+                out=unread_sum[:], in_=x_tiles[t][:], func=ACT.Identity, scale=-1.0 / C_IN, accum_out=stat[:, 0:1]
             )
-            moments[t] = moment
+            stats[t] = stat
 
         def ln_var(t):
-            moment = moments[t]
             unread_sq = work.tile([P, C_IN], BF16)
-            sq_sum = stat_pool.tile([P, 1], F32)
             nc.scalar.activation(
-                out=unread_sq[:], in_=x_tiles[t][:], func=ACT.Square, bias=moment[:, 0:1], accum_out=sq_sum[:]
+                out=unread_sq[:],
+                in_=x_tiles[t][:],
+                func=ACT.Square,
+                bias=stats[t][:, 0:1],
+                accum_out=stats[t][:, 1:2],
             )
-            nc.gpsimd.tensor_scalar(
-                out=moment[:, 1:2], in0=sq_sum[:], scalar1=1.0 / C_IN, scalar2=LN_EPS, op0=ALU.mult, op1=ALU.add
+
+        def ln_rstd(t):
+            nc.scalar.activation(
+                out=stats[t][:, 2:3],
+                in_=stats[t][:, 1:2],
+                func=ACT.Abs_reciprocal_sqrt,
+                scale=1.0 / C_IN,
+                bias=LN_EPS,
             )
-            nc.gpsimd.tensor_tensor(out=moment[:, 2:3], in0=moment[:, 1:2], in1=neg_half[:], op=ALU.pow)
-            nc.gpsimd.tensor_tensor(out=moment[:, 3:4], in0=moment[:, 0:1], in1=moment[:, 2:3], op=ALU.mult)
 
         def ln_norm(t):
-            moment = moments[t]
             x_hat = work.tile([P, PACK, P], F32)
-            nc.scalar.activation(
-                out=x_hat[:], in_=x_tiles[t][:].rearrange("r (p u) -> r u p", u=PACK), func=ACT.Identity, scale=moment[:, 2:3], bias=moment[:, 3:4]
+            nc.gpsimd.tensor_scalar(
+                out=x_hat[:],
+                in0=x_tiles[t][:].rearrange("r (p u) -> r u p", u=PACK),
+                scalar1=stats[t][:, 0:1],
+                scalar2=stats[t][:, 2:3],
+                op0=ALU.add,
+                op1=ALU.mult,
             )
             x_hats[t] = x_hat
 
@@ -361,67 +371,76 @@ def tile_templatepairembeddermultimer_pa_t_kernel(
                 )
             products[t] = product
 
-        def feat_transpose(t):
-            side = psum_one.tile([P, 1 + SUMMED_TERMS, P], F32)
-            nc.tensor.transpose(side[:, 0, :], feat[:, t, :], ident[:])
-            for s in range(SUMMED_TERMS):
-                k = K_W + CHAINED_TERMS + s
-                nc.tensor.transpose(side[:, 1 + s, :], feat[:, t, k : k + 1].to_broadcast([P, P]), ident[:])
-            sides[t] = side
+        def spread_weights(term, first_pair, pairs):
+            g, offset = divmod(first_pair, GROUP)
+            return spread_tiles[g][:, term - SPREAD_FIRST, offset : offset + pairs]
 
-        def feat_copy(t):
-            feat_t = work.tile([P, P], F32)
-            nc.scalar.copy(out=feat_t[:], in_=sides[t][:, 0, :])
-            feat_ts[t] = feat_t
+        def pool_term(pair, chunks):
+            if pair not in pool_sums:
+                pool_sum = work.tile([P, VEC_CHUNKS, PAIR_COLS], F32)
+                pool_sums[pair] = pool_sum
+            for c in chunks:
+                nc.gpsimd.tensor_scalar(
+                    out=pool_sums[pair][:, c, :],
+                    in0=spread_weights(POOL_TERM, pair * PAIR_COLS, PAIR_COLS),
+                    scalar1=w_cols[:, c, POOL_TERM : POOL_TERM + 1],
+                    scalar2=0.0,
+                    op0=ALU.mult,
+                    op1=ALU.add,
+                )
 
-        def multiply(t):
-            summand = work.tile([P, SUMMED_TERMS, VEC_CHUNKS, P], F32)
+        def scalar_term(pair, chunks):
+            if pair not in scalar_sums:
+                scalar_sum = work.tile([P, VEC_CHUNKS, PAIR_COLS], F32)
+                scalar_sums[pair] = scalar_sum
+            for c in chunks:
+                nc.scalar.activation(
+                    out=scalar_sums[pair][:, c, :],
+                    in_=spread_weights(SCALAR_TERM, pair * PAIR_COLS, PAIR_COLS),
+                    func=ACT.Identity,
+                    scale=w_cols[:, c, SCALAR_TERM : SCALAR_TERM + 1],
+                )
+
+        def biased_term(t):
+            biased_sum = work.tile([P, VEC_CHUNKS, P], F32)
             for c in range(VEC_CHUNKS):
                 for h in range(2):
                     i = 2 * t + h
                     nc.scalar.activation(
-                        out=summand[:, 0, c, h * N_RES : (h + 1) * N_RES],
-                        in_=sides[t][:, 1, h * N_RES : (h + 1) * N_RES],
+                        out=biased_sum[:, c, h * N_RES : (h + 1) * N_RES],
+                        in_=spread_weights(BIASED_TERM, i * N_RES, N_RES),
                         func=ACT.Identity,
-                        scale=w_cols[:, c, CHAINED_TERMS : CHAINED_TERMS + 1],
+                        scale=w_cols[:, c, BIASED_TERM : BIASED_TERM + 1],
                         bias=b_cols[:, c, i : i + 1],
                     )
-                for s in range(1, SUMMED_TERMS):
-                    nc.scalar.activation(
-                        out=summand[:, s, c, :],
-                        in_=sides[t][:, 1 + s, :],
-                        func=ACT.Identity,
-                        scale=w_cols[:, c, CHAINED_TERMS + s : CHAINED_TERMS + s + 1],
-                    )
-            summands[t] = summand
+            biased_sums[t] = biased_sum
 
         def sum_chunks(t, chunks):
+            half = slice((t % 2) * P, (t % 2 + 1) * P)
             for c in chunks:
-                chunk = slice(PLAIN_COLS + c * P, PLAIN_COLS + (c + 1) * P)
-                nc.tensor.matmul(
-                    out=extras[t][:, chunk],
-                    lhsT=a_twice[:, c, :, :].rearrange("p h j -> p (h j)"),
-                    rhs=ident[:],
-                    is_transpose=True,
-                    start=True,
-                    stop=False,
+                summands = (
+                    a_twice[:, c, :, :].rearrange("p h j -> p (h j)"),
+                    pool_sums[t // 2][:, c, half],
+                    scalar_sums[t // 2][:, c, half],
+                    biased_sums[t][:, c, :],
                 )
-                for s in range(SUMMED_TERMS):
+                for s, summand in enumerate(summands):
                     nc.tensor.matmul(
-                        out=extras[t][:, chunk],
-                        lhsT=summands[t][:, s, c, :],
+                        out=extras[t][:, PLAIN_COLS + c * P : PLAIN_COLS + (c + 1) * P],
+                        lhsT=summand,
                         rhs=ident[:],
                         is_transpose=True,
-                        start=False,
-                        stop=(s == SUMMED_TERMS - 1),
+                        start=(s == 0),
+                        stop=(s == len(summands) - 1),
                     )
 
         def plain_piece(t, piece):
             cols = slice(piece * PIECE_COLS, (piece + 1) * PIECE_COLS)
+            first = (t % HALF_TILES) * P
             nc.tensor.matmul(
                 out=extras[t][:, cols],
-                lhsT=feat_ts[t][:],
-                rhs=table[:, t // (TILES // 2), cols],
+                lhsT=feat_t[:, first : first + P],
+                rhs=table[:, t // HALF_TILES, cols],
                 start=True,
                 stop=True,
             )
@@ -439,14 +458,17 @@ def tile_templatepairembeddermultimer_pa_t_kernel(
             sum_chunks(t, (1, 0))
             plain_piece(t, 1)
 
+        def weight_col(term, t):
+            return weight_cols[:, term * TILES + t : term * TILES + t + 1]
+
         def combine_open(t):
             result = res_pool.tile([P, C_OUT], F32)
             partial = work.tile([P, VEC_COLS], F32)
             first, second = slice(0, BANK), slice(BANK, C_OUT)
             nc.vector.scalar_tensor_tensor(
                 out=partial[:, BANK - PLAIN_COLS : VEC_COLS],
-                in0=w_all[:, 0, BANK - PLAIN_COLS : VEC_COLS],
-                scalar=feat[:, t, K_W : K_W + 1],
+                in0=open_row[:, BANK - PLAIN_COLS : VEC_COLS],
+                scalar=weight_col(OPEN_TERM, t),
                 in1=products[t][:, second],
                 op0=ALU.mult,
                 op1=ALU.add,
@@ -455,8 +477,8 @@ def tile_templatepairembeddermultimer_pa_t_kernel(
             nc.vector.tensor_tensor(out=result[:, second], in0=act_tiles[t][:, second], in1=extras[t][:, second], op=ALU.add)
             nc.vector.scalar_tensor_tensor(
                 out=partial[:, 0 : BANK - PLAIN_COLS],
-                in0=w_all[:, 0, 0 : BANK - PLAIN_COLS],
-                scalar=feat[:, t, K_W : K_W + 1],
+                in0=open_row[:, 0 : BANK - PLAIN_COLS],
+                scalar=weight_col(OPEN_TERM, t),
                 in1=extras[t][:, PLAIN_COLS:BANK],
                 op0=ALU.mult,
                 op1=ALU.add,
@@ -467,17 +489,15 @@ def tile_templatepairembeddermultimer_pa_t_kernel(
             results[t] = result
             partials[t] = partial
 
-        def combine_rank_one(t):
-            for f in range(1, CHAINED_TERMS):
-                running = results[t][:, PLAIN_COLS:C_OUT] if f % 2 == 1 else partials[t][:]
-                nc.vector.scalar_tensor_tensor(
-                    out=running,
-                    in0=w_all[:, f, :],
-                    scalar=feat[:, t, K_W + f : K_W + f + 1],
-                    in1=running,
-                    op0=ALU.mult,
-                    op1=ALU.add,
-                )
+        def combine_chain(t):
+            nc.vector.scalar_tensor_tensor(
+                out=partials[t][:],
+                in0=chain_row[:],
+                scalar=weight_col(CHAIN_TERM, t),
+                in1=partials[t][:],
+                op0=ALU.mult,
+                op1=ALU.add,
+            )
 
         def combine_close(t):
             nc.gpsimd.tensor_tensor(
@@ -491,25 +511,116 @@ def tile_templatepairembeddermultimer_pa_t_kernel(
             if 0 <= t < TILES:
                 stage(t)
 
-        for n in range(-6, TILES + 1):
-            if n >= 0:
+        w_grouped = setup.tile([P, C_OUT, PACK], BF16, align_bytes=64)
+
+        def regroup_weights():
+            for b, copy in ((0, nc.vector.tensor_copy), (1, nc.scalar.copy)):
+                cols = slice(b * BANK, (b + 1) * BANK)
+                copy(
+                    out=w_grouped[:, cols, :].rearrange("p (c i) u -> p c u i", i=4),
+                    in_=w_raw[:, :, cols].rearrange("p u (c i) -> p c u i", i=4),
+                )
+
+        def quantise_weights(b):
+            cols = slice(b * BANK, (b + 1) * BANK)
+            nc.vector.quantize_mx(
+                out=w_codes[:, cols].bitcast(FP8X4),
+                scales=w_scales[:, cols],
+                in_=w_grouped[:, cols, :].rearrange("p c u -> p (c u)"),
+            )
+
+        def channel_tables():
+            cols_sum = setup.tile([P, VEC_COLS], F32)
+            nc.vector.tensor_tensor(out=cols_sum[:], in0=cols_a[:], in1=cols_e[:], op=ALU.add)
+            small_t = psum_two.tile([P, VEC_CHUNKS, P], BF16, tag="extra")
+            for c in range(VEC_CHUNKS):
+                nc.tensor.transpose(
+                    small_t[:, c, :], small_rows[:, PLAIN_COLS + c * P : PLAIN_COLS + (c + 1) * P], ident_bf[:]
+                )
+            nc.vector.tensor_copy(out=w_cols[:], in_=small_t[:, :, K_W:K_ONE])
+            w_cols_bf = setup.tile([P, VEC_CHUNKS, 2], BF16)
+            nc.vector.tensor_copy(out=w_cols_bf[:], in_=small_t[:, :, K_W : K_W + 2])
+            bias_sums = setup.tile([P, VEC_CHUNKS], F32)
+            nc.vector.reduce_sum(out=bias_sums[:], in_=small_t[:, :, K_ONE:K_END], axis=mybir.AxisListType.X)
+            cols_t = psum_two.tile([P, VEC_CHUNKS, P], F32, tag="extra")
+            for c in range(VEC_CHUNKS):
+                nc.tensor.transpose(cols_t[:, c, :], cols_sum[:, c * P : (c + 1) * P], ident[:])
+            for chunks in (slice(0, 4), slice(4, 5)):
+                n_chunks = chunks.stop - chunks.start
+                nc.scalar.copy(
+                    out=a_twice[:, chunks, :, :],
+                    in_=cols_t[:, chunks, 0:N_RES].unsqueeze(2).to_broadcast([P, n_chunks, 2, N_RES]),
+                )
+            for c in range(VEC_CHUNKS):
+                nc.scalar.activation(
+                    out=b_cols[:, c, :], in_=cols_t[:, c, N_RES:P], func=ACT.Identity, bias=bias_sums[:, c : c + 1]
+                )
+            open_row_ps = psum_two.tile([P, VEC_COLS], BF16, tag="extra")
+            for c in range(VEC_CHUNKS):
+                for term, row in ((OPEN_TERM, open_row_ps), (CHAIN_TERM, chain_row)):
+                    nc.tensor.transpose(
+                        row[:, c * P : (c + 1) * P], w_cols_bf[:, c, term : term + 1].to_broadcast([P, P]), ident_bf[:]
+                    )
+            nc.scalar.copy(out=open_row[:], in_=open_row_ps[:])
+
+        def weight_columns():
+            weight_cols_ps = psum_two.tile([P, P], F32, tag="extra")
+            nc.tensor.transpose(weight_cols_ps[:], weight_rows[:], ident[:])
+            nc.vector.tensor_copy(out=weight_cols[:], in_=weight_cols_ps[:])
+
+        def plain_table():
+            nc.vector.tensor_tensor(out=table[0:K_W, :, :], in0=table_a[:], in1=table_e[:], op=ALU.add)
+            nc.vector.tensor_copy(
+                out=table[K_W:P, :, :],
+                in_=small_rows[K_W:P, 0:PLAIN_COLS].unsqueeze(1).to_broadcast([P - K_W, 2, PLAIN_COLS]),
+            )
+
+        for n in range(-5, TILES + 1):
+            if n >= -1:
                 each(load_x, n + X_AHEAD)
+            if n >= 0:
                 each(load_act, n + ACT_AHEAD)
+            if n >= 2 and n % GROUP_TILES == 2 and n // GROUP_TILES + 2 < PAIRS // GROUP:
+                load_spread(n // GROUP_TILES + 2)
+            if n == 8 or n == 16:
+                load_features(HALF_TILES + n - 8, 8)
+            each(quantise, n + 1)
+            each(regroup, n + 2)
             each(combine_close, n - 1)
             each(store, n - 1)
-            each(ln_affine, n + 2)
-            each(feat_copy, n + 2)
-            each(multiply, n + 2)
-            each(ln_norm, n + 4)
-            each(ln_var, n + 5)
-            each(ln_sum, n + 6)
+            if n == -3:
+                regroup_weights()
+                quantise_weights(0)
+            each(ln_var, n + 4)
+            each(ln_sum, n + 5)
+            each(ln_rstd, n + 4)
+            if n >= -1:
+                each(biased_term, n + 2)
+                if n % 2 == 1 and n + 3 < TILES:
+                    scalar_term((n + 3) // 2, (4, 3, 2))
+                if n % 2 == 0 and n + 2 < TILES:
+                    scalar_term((n + 2) // 2, (1, 0))
             each(combine_open, n)
-            each(small_terms_first, n + 1)
+            each(ln_norm, n + 4)
             each(ln_transpose, n + 3)
+            each(ln_affine, n + 3)
+            if n == -3:
+                quantise_weights(1)
+                channel_tables()
+                plain_table()
+            if n == -2:
+                biased_term(0)
+                scalar_term(0, (4, 3, 2, 1, 0))
+                pool_term(0, (4, 3, 2, 1, 0))
+            if n >= -1:
+                if n % 2 == 1 and n + 3 < TILES:
+                    pool_term((n + 3) // 2, (4, 3, 2))
+                if n % 2 == 0 and n + 2 < TILES:
+                    pool_term((n + 2) // 2, (1, 0))
+            if n == -1:
+                weight_columns()
+            each(small_terms_first, n + 1)
             each(small_terms_second, n + 1)
             each(project, n + 1)
             each(small_terms_third, n + 1)
-            each(feat_transpose, n + 3)
-            each(regroup, n + 2)
-            each(combine_rank_one, n)
-            each(quantise, n + 2)
+            each(combine_chain, n)

@@ -128,36 +128,69 @@ def tile_templatepairembeddermultimer_pa_t_kernel(
             )
             spread_tiles[g] = spread
 
+        mask_rows = setup.tile([P, 3, N_RES], BF16)
+        for m, mask in enumerate((backbone_mask, pseudo_beta_mask)):
+            nc.sync.dma_start(out=mask_rows[:, m, :], in_=mask.partition_broadcast(P))
+        multichain = setup.tile([N_RES, N_RES], BF16)
+        nc.sync.dma_start(out=multichain[:], in_=multichain_mask_2d[:, :])
+        units = setup.tile([N_RES, 3, N_RES], BF16)
+        for u, unit in enumerate((unit_x, unit_y, unit_z)):
+            nc.sync.dma_start(out=units[:, u, :], in_=unit[:, :])
         load_x(0)
-        vec_rows = setup.tile([P, P], BF16)
-        nc.vector.memset(vec_rows[:], 0.0)
-        residue_masks = (backbone_mask, pseudo_beta_mask)
-        for m in range(2):
-            nc.sync.dma_start(
-                out=vec_rows[m : m + 1, :].rearrange("o (h j) -> o h j", h=2),
-                in_=residue_masks[m].unsqueeze(0).unsqueeze(0).to_broadcast([1, 2, N_RES]),
-            )
-        mask_rows = setup.tile([P, 2, N_RES], BF16)
-        for m in range(2):
-            nc.sync.dma_start(out=mask_rows[:, m, :], in_=residue_masks[m].partition_broadcast(P))
-        multichain = setup.tile([P, N_RES], BF16)
-        units = setup.tile([P, 2, N_RES], BF16)
-        for b in range(2):
-            nc.sync.dma_start(out=multichain[b * N_RES : (b + 1) * N_RES, :], in_=multichain_mask_2d[:, :])
-        nc.sync.dma_start(out=units[0:N_RES, 0, :], in_=unit_x[:, :])
-        nc.sync.dma_start(out=units[N_RES:P, 0, :], in_=unit_y[:, :])
-        nc.sync.dma_start(out=units[0:N_RES, 1, :], in_=unit_z[:, :])
-        nc.vector.memset(units[N_RES:P, 1, :], 1.0)
         load_x(1)
-        w_raw = setup.tile([P, PACK, C_OUT], BF16)
-        for b in range(BANKS):
-            cols = slice(b * BANK, (b + 1) * BANK)
-            nc.sync.dma_start(out=w_raw[:, :, cols], in_=w_q.rearrange("(p u) c -> p u c", u=PACK)[:, :, cols])
         gain_raw = setup.tile([P, PACK], BF16)
         nc.sync.dma_start(out=gain_raw[:], in_=ln_g.rearrange("(p u) -> p u", u=PACK))
         shift_raw = setup.tile([P, PACK], BF16)
         nc.sync.dma_start(out=shift_raw[:], in_=ln_b.rearrange("(p u) -> p u", u=PACK))
-        load_x(2)
+        w_raw = setup.tile([P, PACK, C_OUT], BF16)
+
+        def load_weights(b):
+            cols = slice(b * BANK, (b + 1) * BANK)
+            nc.sync.dma_start(out=w_raw[:, :, cols], in_=w_q.rearrange("(p u) c -> p u c", u=PACK)[:, :, cols])
+
+        load_weights(0)
+
+        one_col = const.tile([P, 1], F32)
+        nc.vector.memset(one_col[:], 1.0)
+        unread_one = const.tile([P, 1], F32)
+        nc.scalar.activation(out=unread_one[:], in_=one_col[:], func=ACT.Abs_reciprocal_sqrt)
+        small_rows = setup.tile([P, C_OUT], BF16)
+        nc.vector.memset(small_rows[:], 0.0)
+        for r, row in enumerate(rank_one_rows):
+            nc.sync.dma_start(out=small_rows[K_W + r : K_W + r + 1, :], in_=row[:, :])
+        feat_t = const.tile([P, HALF_PAIRS], F32)
+        nc.vector.memset(feat_t[K_W:P, :], 1.0)
+        ident_bf = const.tile([P, P], BF16)
+        make_identity(nc, ident_bf[:])
+        ident = const.tile([P, P], F32)
+        make_identity(nc, ident[:])
+
+        nc.vector.tensor_copy(out=mask_rows[:, 2, :], in_=mask_rows[:, 0, :])
+        mask_cols_ps = psum_two.tile([P, 2, P], BF16, tag="extra")
+        for m in range(2):
+            nc.tensor.transpose(
+                mask_cols_ps[:, m, :], mask_rows[:, m : m + 2, :].rearrange("p m j -> p (m j)"), ident_bf[:]
+            )
+        mask_cols = setup.tile([N_RES, 2], F32)
+        nc.vector.tensor_copy(out=mask_cols[:], in_=mask_cols_ps[0:N_RES, :, 0])
+        weights = setup.tile([N_RES, N_W, N_RES], F32)
+        for m in range(2):
+            nc.vector.scalar_tensor_tensor(
+                out=weights[:, BIASED_TERM + m, :],
+                in0=multichain[:],
+                scalar=mask_cols[:, m : m + 1],
+                in1=mask_rows[0:N_RES, m, :],
+                op0=ALU.mult,
+                op1=ALU.mult,
+            )
+        nc.vector.tensor_tensor(
+            out=weights[:, 0:BIASED_TERM, :],
+            in0=units[:],
+            in1=weights[:, BIASED_TERM : BIASED_TERM + 1, :].to_broadcast([N_RES, BIASED_TERM, N_RES]),
+            op=ALU.mult,
+        )
+        nc.sync.dma_start(out=scratch.rearrange("s (i j) -> i s j", j=N_RES), in_=weights[:])
+        load_weights(1)
 
         cols_a = setup.tile([P, VEC_COLS], BF16)
         cols_e = setup.tile([P, VEC_COLS], BF16)
@@ -165,12 +198,24 @@ def tile_templatepairembeddermultimer_pa_t_kernel(
         nc.sync.dma_start(out=cols_a[N_RES:P, :], in_=aa_proj2[:, PLAIN_COLS:C_OUT])
         nc.sync.dma_start(out=cols_e[0:N_RES, :], in_=esm_proj1[:, PLAIN_COLS:C_OUT])
         nc.sync.dma_start(out=cols_e[N_RES:P, :], in_=esm_proj2[:, PLAIN_COLS:C_OUT])
-        small_rows = setup.tile([P, C_OUT], BF16)
-        nc.vector.memset(small_rows[:], 0.0)
-        for r, row in enumerate(rank_one_rows):
-            nc.sync.dma_start(out=small_rows[K_W + r : K_W + r + 1, :], in_=row[:, :])
         for r, row in enumerate(bias_rows):
             nc.sync.dma_start(out=small_rows[K_ONE + r : K_ONE + r + 1, :], in_=row.unsqueeze(0))
+        load_x(2)
+        load_spread(0)
+        weight_rows = setup.tile([P, P], F32)
+        nc.sync.dma_start(
+            out=weight_rows[:], in_=scratch[0 : P // TILES, :].rearrange("s (t p) -> (s t) p", p=P)
+        )
+        load_x(3)
+
+        def load_features(first_tile, tiles):
+            first = first_tile * P
+            nc.sync.dma_start(
+                out=feat_t[K_W:K_ONE, first % HALF_PAIRS : first % HALF_PAIRS + tiles * P],
+                in_=scratch[:, first : first + tiles * P],
+            )
+
+        load_features(0, HALF_TILES)
         table_a = setup.tile([K_W, 2, PLAIN_COLS], BF16)
         table_e = setup.tile([K_W, 2, PLAIN_COLS], BF16)
         for tab, by_j, by_i in ((table_a, aa_proj1, aa_proj2), (table_e, esm_proj1, esm_proj2)):
@@ -181,19 +226,23 @@ def tile_templatepairembeddermultimer_pa_t_kernel(
             nc.sync.dma_start(
                 out=tab[K_I : K_I + I_HALF, :, :], in_=by_i.rearrange("(s m) c -> m s c", s=2)[:, :, 0:PLAIN_COLS]
             )
+        load_act(0)
+        load_x(4)
+        load_act(1)
+        load_spread(1)
+        load_x(5)
+        load_act(2)
+        load_x(6)
 
-        ident = const.tile([P, P], F32)
-        make_identity(nc, ident[:])
-        ident_bf = const.tile([P, P], BF16)
-        make_identity(nc, ident_bf[:])
-
-        feat_t = const.tile([P, HALF_PAIRS], F32)
-        nc.vector.memset(feat_t[K_W:P, :], 1.0)
-        nc.scalar.copy(
+        vec_cols = const.tile([P, 2 * PACK], F32)
+        nc.vector.tensor_copy(out=vec_cols[:, 0:PACK], in_=gain_raw[:])
+        nc.vector.tensor_copy(out=vec_cols[:, PACK : 2 * PACK], in_=shift_raw[:])
+        nc.vector.tensor_copy(
             out=feat_t[K_J : K_J + N_RES, :].rearrange("k (i j) -> k i j", j=N_RES),
             in_=ident[0:N_RES, 0:N_RES].unsqueeze(1).to_broadcast([N_RES, I_HALF, N_RES]),
         )
-        for q in range(4):
+
+        def one_hot_i(q):
             i_cols = slice(K_I + q * 8, K_I + (q + 1) * 8)
             nc.gpsimd.tensor_scalar(
                 out=feat_t[K_I : K_I + I_HALF, q * GROUP : (q + 1) * GROUP].rearrange("k (i j) -> k i j", j=N_RES),
@@ -204,57 +253,7 @@ def tile_templatepairembeddermultimer_pa_t_kernel(
                 op1=ALU.add,
             )
 
-        vec_cols_ps = psum_two.tile([P, P], BF16, tag="extra")
-        nc.tensor.transpose(vec_cols_ps[:], vec_rows[:], ident_bf[:])
-        mask_cols = const.tile([P, 2], F32)
-        nc.vector.tensor_copy(out=mask_cols[:], in_=vec_cols_ps[:, 0:2])
-        pair_masks = setup.tile([P, 2, N_RES], F32)
-        for m in range(2):
-            nc.vector.scalar_tensor_tensor(
-                out=pair_masks[:, m, :],
-                in0=multichain[:],
-                scalar=mask_cols[:, m : m + 1],
-                in1=mask_rows[:, m, :],
-                op0=ALU.mult,
-                op1=ALU.mult,
-            )
-        weights = setup.tile([P, 2, N_RES], F32)
-        nc.vector.tensor_tensor(
-            out=weights[:], in0=units[:], in1=pair_masks[:, 0:1, :].to_broadcast([P, 2, N_RES]), op=ALU.mult
-        )
-        for g in range(2):
-            nc.sync.dma_start(
-                out=scratch[2 * g : 2 * g + 2, :].rearrange("b (i j) -> (b i) j", j=N_RES), in_=weights[:, g, :]
-            )
-        nc.sync.dma_start(
-            out=scratch[N_W - 1 : N_W, :].rearrange("b (i j) -> (b i) j", j=N_RES), in_=pair_masks[0:N_RES, 1, :]
-        )
-        load_spread(0)
-        weight_rows = setup.tile([P, P], F32)
-        nc.sync.dma_start(
-            out=weight_rows[:], in_=scratch[0 : P // TILES, :].rearrange("s (t p) -> (s t) p", p=P)
-        )
-
-        def load_features(first_tile, tiles):
-            first = first_tile * P
-            nc.sync.dma_start(
-                out=feat_t[K_W:K_ONE, first % HALF_PAIRS : first % HALF_PAIRS + tiles * P],
-                in_=scratch[:, first : first + tiles * P],
-            )
-
-        load_features(0, HALF_TILES)
-        load_x(3)
-        load_x(4)
-        load_act(0)
-        load_act(1)
-        load_spread(1)
-        load_x(5)
-        load_act(2)
-        load_x(6)
-
-        vec_cols = const.tile([P, 2 * PACK], F32)
-        nc.vector.tensor_copy(out=vec_cols[:, 0:PACK], in_=gain_raw[:])
-        nc.vector.tensor_copy(out=vec_cols[:, PACK : 2 * PACK], in_=shift_raw[:])
+        one_hot_i(0)
 
         stats = {}
         x_hats = {}
@@ -513,13 +512,12 @@ def tile_templatepairembeddermultimer_pa_t_kernel(
 
         w_grouped = setup.tile([P, C_OUT, PACK], BF16, align_bytes=64)
 
-        def regroup_weights():
-            for b, copy in ((0, nc.vector.tensor_copy), (1, nc.scalar.copy)):
-                cols = slice(b * BANK, (b + 1) * BANK)
-                copy(
-                    out=w_grouped[:, cols, :].rearrange("p (c i) u -> p c u i", i=4),
-                    in_=w_raw[:, :, cols].rearrange("p u (c i) -> p c u i", i=4),
-                )
+        def regroup_weights(b):
+            cols = slice(b * BANK, (b + 1) * BANK)
+            nc.vector.tensor_copy(
+                out=w_grouped[:, cols, :].rearrange("p (c i) u -> p c u i", i=4),
+                in_=w_raw[:, :, cols].rearrange("p u (c i) -> p c u i", i=4),
+            )
 
         def quantise_weights(b):
             cols = slice(b * BANK, (b + 1) * BANK)
@@ -529,28 +527,33 @@ def tile_templatepairembeddermultimer_pa_t_kernel(
                 in_=w_grouped[:, cols, :].rearrange("p c u -> p (c u)"),
             )
 
-        def channel_tables():
-            cols_sum = setup.tile([P, VEC_COLS], F32)
-            nc.vector.tensor_tensor(out=cols_sum[:], in0=cols_a[:], in1=cols_e[:], op=ALU.add)
-            small_t = psum_two.tile([P, VEC_CHUNKS, P], BF16, tag="extra")
-            for c in range(VEC_CHUNKS):
-                nc.tensor.transpose(
-                    small_t[:, c, :], small_rows[:, PLAIN_COLS + c * P : PLAIN_COLS + (c + 1) * P], ident_bf[:]
-                )
-            nc.vector.tensor_copy(out=w_cols[:], in_=small_t[:, :, K_W:K_ONE])
-            w_cols_bf = setup.tile([P, VEC_CHUNKS, 2], BF16)
-            nc.vector.tensor_copy(out=w_cols_bf[:], in_=small_t[:, :, K_W : K_W + 2])
-            bias_sums = setup.tile([P, VEC_CHUNKS], F32)
-            nc.vector.reduce_sum(out=bias_sums[:], in_=small_t[:, :, K_ONE:K_END], axis=mybir.AxisListType.X)
+        cols_sum = setup.tile([P, VEC_COLS], F32)
+        w_cols_bf = setup.tile([P, VEC_CHUNKS, 2], BF16)
+        bias_sums = setup.tile([P, VEC_CHUNKS], F32)
+
+        def residue_tables_transpose():
             cols_t = psum_two.tile([P, VEC_CHUNKS, P], F32, tag="extra")
             for c in range(VEC_CHUNKS):
                 nc.tensor.transpose(cols_t[:, c, :], cols_sum[:, c * P : (c + 1) * P], ident[:])
+            return cols_t
+
+        def residue_tables_copy(cols_t):
             for chunks in (slice(0, 4), slice(4, 5)):
                 n_chunks = chunks.stop - chunks.start
                 nc.scalar.copy(
                     out=a_twice[:, chunks, :, :],
                     in_=cols_t[:, chunks, 0:N_RES].unsqueeze(2).to_broadcast([P, n_chunks, 2, N_RES]),
                 )
+
+        def channel_tables(cols_t):
+            small_t = psum_two.tile([P, VEC_CHUNKS, P], BF16, tag="extra")
+            for c in range(VEC_CHUNKS):
+                nc.tensor.transpose(
+                    small_t[:, c, :], small_rows[:, PLAIN_COLS + c * P : PLAIN_COLS + (c + 1) * P], ident_bf[:]
+                )
+            nc.vector.tensor_copy(out=w_cols_bf[:], in_=small_t[:, :, K_W : K_W + 2])
+            nc.vector.reduce_sum(out=bias_sums[:], in_=small_t[:, :, K_ONE:K_END], axis=mybir.AxisListType.X)
+            nc.vector.tensor_copy(out=w_cols[:], in_=small_t[:, :, K_W:K_ONE])
             for c in range(VEC_CHUNKS):
                 nc.scalar.activation(
                     out=b_cols[:, c, :], in_=cols_t[:, c, N_RES:P], func=ACT.Identity, bias=bias_sums[:, c : c + 1]
@@ -561,7 +564,7 @@ def tile_templatepairembeddermultimer_pa_t_kernel(
                     nc.tensor.transpose(
                         row[:, c * P : (c + 1) * P], w_cols_bf[:, c, term : term + 1].to_broadcast([P, P]), ident_bf[:]
                     )
-            nc.scalar.copy(out=open_row[:], in_=open_row_ps[:])
+            return open_row_ps
 
         def weight_columns():
             weight_cols_ps = psum_two.tile([P, P], F32, tag="extra")
@@ -575,50 +578,87 @@ def tile_templatepairembeddermultimer_pa_t_kernel(
                 in_=small_rows[K_W:P, 0:PLAIN_COLS].unsqueeze(1).to_broadcast([P - K_W, 2, PLAIN_COLS]),
             )
 
-        for n in range(-5, TILES + 1):
-            if n >= -1:
-                each(load_x, n + X_AHEAD)
+        def first_scalar_term():
+            scalar_sum = work.tile([P, VEC_CHUNKS, PAIR_COLS], F32)
+            for c in range(VEC_CHUNKS):
+                nc.vector.tensor_scalar(
+                    out=scalar_sum[:, c, :],
+                    in0=spread_weights(SCALAR_TERM, 0, PAIR_COLS),
+                    scalar1=w_cols[:, c, SCALAR_TERM : SCALAR_TERM + 1],
+                    scalar2=None,
+                    op0=ALU.mult,
+                )
+            scalar_sums[0] = scalar_sum
+
+        every_chunk = (4, 3, 2, 1, 0)
+        ln_sum(0)
+        ln_var(0)
+        ln_sum(1)
+        ln_rstd(0)
+        ln_norm(0)
+        ln_transpose(0)
+        ln_var(1)
+        ln_rstd(1)
+        ln_norm(1)
+        regroup_weights(0)
+        nc.vector.tensor_tensor(out=cols_sum[:], in0=cols_a[:], in1=cols_e[:], op=ALU.add)
+        cols_t = residue_tables_transpose()
+        quantise_weights(0)
+        ln_affine(0)
+        ln_transpose(1)
+        regroup_weights(1)
+        ln_sum(2)
+        ln_var(2)
+        ln_rstd(2)
+        residue_tables_copy(cols_t)
+        ln_affine(1)
+        open_row_ps = channel_tables(cols_t)
+        quantise_weights(1)
+        regroup(0)
+        for q in range(1, 4):
+            one_hot_i(q)
+        ln_norm(2)
+        ln_transpose(2)
+        biased_term(0)
+        nc.scalar.copy(out=open_row[:], in_=open_row_ps[:])
+        quantise(0)
+        first_scalar_term()
+        weight_columns()
+        plain_table()
+        pool_term(0, every_chunk)
+        regroup(1)
+        ln_affine(2)
+        for n in range(-1, TILES + 1):
+            each(load_x, n + X_AHEAD)
             if n >= 0:
                 each(load_act, n + ACT_AHEAD)
+                each(quantise, n + 1)
+                each(regroup, n + 2)
             if n >= 2 and n % GROUP_TILES == 2 and n // GROUP_TILES + 2 < PAIRS // GROUP:
                 load_spread(n // GROUP_TILES + 2)
             if n == 8 or n == 16:
                 load_features(HALF_TILES + n - 8, 8)
-            each(quantise, n + 1)
-            each(regroup, n + 2)
             each(combine_close, n - 1)
             each(store, n - 1)
-            if n == -3:
-                regroup_weights()
-                quantise_weights(0)
+            if n < 0:
+                each(ln_sum, n + 4)
             each(ln_var, n + 4)
             each(ln_sum, n + 5)
             each(ln_rstd, n + 4)
-            if n >= -1:
-                each(biased_term, n + 2)
-                if n % 2 == 1 and n + 3 < TILES:
-                    scalar_term((n + 3) // 2, (4, 3, 2))
-                if n % 2 == 0 and n + 2 < TILES:
-                    scalar_term((n + 2) // 2, (1, 0))
+            each(biased_term, n + 2)
+            if n % 2 == 1 and n + 3 < TILES:
+                scalar_term((n + 3) // 2, every_chunk[:3])
+            if n % 2 == 0 and n + 2 < TILES:
+                scalar_term((n + 2) // 2, every_chunk[3:])
             each(combine_open, n)
             each(ln_norm, n + 4)
-            each(ln_transpose, n + 3)
-            each(ln_affine, n + 3)
-            if n == -3:
-                quantise_weights(1)
-                channel_tables()
-                plain_table()
-            if n == -2:
-                biased_term(0)
-                scalar_term(0, (4, 3, 2, 1, 0))
-                pool_term(0, (4, 3, 2, 1, 0))
-            if n >= -1:
-                if n % 2 == 1 and n + 3 < TILES:
-                    pool_term((n + 3) // 2, (4, 3, 2))
-                if n % 2 == 0 and n + 2 < TILES:
-                    pool_term((n + 2) // 2, (1, 0))
-            if n == -1:
-                weight_columns()
+            if n >= 0:
+                each(ln_transpose, n + 3)
+                each(ln_affine, n + 3)
+            if n % 2 == 1 and n + 3 < TILES:
+                pool_term((n + 3) // 2, every_chunk[:3])
+            if n % 2 == 0 and n + 2 < TILES:
+                pool_term((n + 2) // 2, every_chunk[3:])
             each(small_terms_first, n + 1)
             each(small_terms_second, n + 1)
             each(project, n + 1)

@@ -354,21 +354,20 @@ def tile_templatepairembeddermultimer_pa_t_kernel(
             )
             q_words[t] = (q_codes, q_scales)
 
-        def project(t):
+        def project(t, bank):
             q_codes, q_scales = q_words[t]
-            product = psum_one.tile([P, C_OUT], F32)
-            for bank in range(BANKS):
-                cols = slice(bank * BANK, (bank + 1) * BANK)
-                nc.tensor.matmul_mx(
-                    out=product[:, cols],
-                    lhsT=q_codes[:].bitcast(FP8X4),
-                    lhsT_scale=q_scales[:],
-                    rhs=w_codes[:, cols].bitcast(FP8X4),
-                    rhs_scale=w_scales[:, cols],
-                    start=True,
-                    stop=True,
-                )
-            products[t] = product
+            cols = slice(bank * BANK, (bank + 1) * BANK)
+            product = psum_one.tile([P, BANK], F32, tag="product%d" % bank)
+            nc.tensor.matmul_mx(
+                out=product[:],
+                lhsT=q_codes[:].bitcast(FP8X4),
+                lhsT_scale=q_scales[:],
+                rhs=w_codes[:, cols].bitcast(FP8X4),
+                rhs_scale=w_scales[:, cols],
+                start=True,
+                stop=True,
+            )
+            products[t, bank] = product
 
         def spread_weights(term, first_pair, pairs):
             g, offset = divmod(first_pair, GROUP)
@@ -449,13 +448,12 @@ def tile_templatepairembeddermultimer_pa_t_kernel(
             extras[t] = extra
             sum_chunks(t, (4, 3))
             plain_piece(t, 0)
+            project(t, 1)
 
         def small_terms_second(t):
-            sum_chunks(t, (2,))
-
-        def small_terms_third(t):
-            sum_chunks(t, (1, 0))
+            sum_chunks(t, (2, 1, 0))
             plain_piece(t, 1)
+            project(t, 0)
 
         def weight_col(term, t):
             return weight_cols[:, term * TILES + t : term * TILES + t + 1]
@@ -468,11 +466,11 @@ def tile_templatepairembeddermultimer_pa_t_kernel(
                 out=partial[:, BANK - PLAIN_COLS : VEC_COLS],
                 in0=open_row[:, BANK - PLAIN_COLS : VEC_COLS],
                 scalar=weight_col(OPEN_TERM, t),
-                in1=products[t][:, second],
+                in1=products[t, 1][:],
                 op0=ALU.mult,
                 op1=ALU.add,
             )
-            nc.vector.tensor_tensor(out=result[:, first], in0=act_tiles[t][:, first], in1=products[t][:, first], op=ALU.add)
+            nc.vector.tensor_tensor(out=result[:, first], in0=act_tiles[t][:, first], in1=products[t, 0][:], op=ALU.add)
             nc.vector.tensor_tensor(out=result[:, second], in0=act_tiles[t][:, second], in1=extras[t][:, second], op=ALU.add)
             nc.vector.scalar_tensor_tensor(
                 out=partial[:, 0 : BANK - PLAIN_COLS],
@@ -661,6 +659,4 @@ def tile_templatepairembeddermultimer_pa_t_kernel(
                 pool_term((n + 2) // 2, every_chunk[3:])
             each(small_terms_first, n + 1)
             each(small_terms_second, n + 1)
-            each(project, n + 1)
-            each(small_terms_third, n + 1)
             each(combine_chain, n)

@@ -44,9 +44,6 @@ GROUP = 512
 GROUP_TILES = GROUP // P
 PAIR_COLS = 2 * P
 
-PLAIN_PIECES = 2
-PIECE_COLS = PLAIN_COLS // PLAIN_PIECES
-
 X_AHEAD = 8
 ACT_AHEAD = 3
 
@@ -308,7 +305,7 @@ def tile_templatepairembeddermultimer_pa_t_kernel(
 
         def ln_norm(t):
             x_hat = work.tile([P, PACK, P], F32)
-            nc.gpsimd.tensor_scalar(
+            nc.vector.tensor_scalar(
                 out=x_hat[:],
                 in0=x_tiles[t][:].rearrange("r (p u) -> r u p", u=PACK),
                 scalar1=stats[t][:, 0:1],
@@ -432,13 +429,12 @@ def tile_templatepairembeddermultimer_pa_t_kernel(
                         stop=(s == len(summands) - 1),
                     )
 
-        def plain_piece(t, piece):
-            cols = slice(piece * PIECE_COLS, (piece + 1) * PIECE_COLS)
+        def plain_matmul(t):
             first = (t % HALF_TILES) * P
             nc.tensor.matmul(
-                out=extras[t][:, cols],
+                out=extras[t][:, 0:PLAIN_COLS],
                 lhsT=feat_t[:, first : first + P],
-                rhs=table[:, t // HALF_TILES, cols],
+                rhs=table[:, t // HALF_TILES, :],
                 start=True,
                 stop=True,
             )
@@ -446,14 +442,13 @@ def tile_templatepairembeddermultimer_pa_t_kernel(
         def small_terms_first(t):
             extra = psum_two.tile([P, C_OUT], F32)
             extras[t] = extra
-            sum_chunks(t, (4, 3))
-            plain_piece(t, 0)
-            project(t, 1)
+            sum_chunks(t, (4, 3, 2))
+            plain_matmul(t)
 
         def small_terms_second(t):
-            sum_chunks(t, (2, 1, 0))
-            plain_piece(t, 1)
-            project(t, 0)
+            sum_chunks(t, (1, 0))
+            for bank in range(BANKS):
+                project(t, BANKS - 1 - bank)
 
         def weight_col(term, t):
             return weight_cols[:, term * TILES + t : term * TILES + t + 1]
@@ -630,8 +625,6 @@ def tile_templatepairembeddermultimer_pa_t_kernel(
             each(load_x, n + X_AHEAD)
             if n >= 0:
                 each(load_act, n + ACT_AHEAD)
-                each(quantise, n + 1)
-                each(regroup, n + 2)
             if n >= 2 and n % GROUP_TILES == 2 and n // GROUP_TILES + 2 < PAIRS // GROUP:
                 load_spread(n // GROUP_TILES + 2)
             if n == 8 or n == 16:
@@ -649,7 +642,11 @@ def tile_templatepairembeddermultimer_pa_t_kernel(
             if n % 2 == 0 and n + 2 < TILES:
                 scalar_term((n + 2) // 2, every_chunk[3:])
             each(combine_open, n)
+            if n >= 0:
+                each(quantise, n + 1)
             each(ln_norm, n + 4)
+            if n >= 0:
+                each(regroup, n + 2)
             if n >= 0:
                 each(ln_transpose, n + 3)
                 each(ln_affine, n + 3)

@@ -40,8 +40,6 @@ OPEN_TERM, CHAIN_TERM, POOL_TERM, BIASED_TERM, SCALAR_TERM = range(N_W)
 SPREAD_FIRST = POOL_TERM
 N_SPREAD = N_W - SPREAD_FIRST
 
-GROUP = 512
-GROUP_TILES = GROUP // P
 PAIR_COLS = 2 * P
 
 X_AHEAD = 8
@@ -97,7 +95,7 @@ def tile_templatepairembeddermultimer_pa_t_kernel(
         x_pool = stack.enter_context(tc.tile_pool(name="x", bufs=X_AHEAD))
         act_pool = stack.enter_context(tc.tile_pool(name="act", bufs=ACT_AHEAD + 2))
         stat_pool = stack.enter_context(tc.tile_pool(name="stat", bufs=8))
-        spread_pool = stack.enter_context(tc.tile_pool(name="spread", bufs=3))
+        spread_pool = stack.enter_context(tc.tile_pool(name="spread", bufs=5))
         work = stack.enter_context(tc.tile_pool(name="work", bufs=3))
         res_pool = stack.enter_context(tc.tile_pool(name="res", bufs=4))
         psum_two = stack.enter_context(tc.psum_pool(name="psum_two", bufs=2))
@@ -118,139 +116,19 @@ def tile_templatepairembeddermultimer_pa_t_kernel(
             act_tiles[t] = act_tile
 
         def load_spread(g):
-            spread = spread_pool.tile([P, N_SPREAD, GROUP], F32)
+            spread = spread_pool.tile([P, N_SPREAD, PAIR_COLS], F32)
             nc.sync.dma_start(
                 out=spread[:],
-                in_=scratch[SPREAD_FIRST:N_W, g * GROUP : (g + 1) * GROUP].partition_broadcast(P),
+                in_=scratch[SPREAD_FIRST:N_W, g * PAIR_COLS : (g + 1) * PAIR_COLS].partition_broadcast(P),
             )
             spread_tiles[g] = spread
 
-        mask_rows = setup.tile([P, 3, N_RES], BF16)
-        for m, mask in enumerate((backbone_mask, pseudo_beta_mask)):
-            nc.sync.dma_start(out=mask_rows[:, m, :], in_=mask.partition_broadcast(P))
-        multichain = setup.tile([N_RES, N_RES], BF16)
-        nc.sync.dma_start(out=multichain[:], in_=multichain_mask_2d[:, :])
-        units = setup.tile([N_RES, 3, N_RES], BF16)
-        for u, unit in enumerate((unit_x, unit_y, unit_z)):
-            nc.sync.dma_start(out=units[:, u, :], in_=unit[:, :])
-        load_x(0)
-        load_x(1)
-        gain_raw = setup.tile([P, PACK], BF16)
-        nc.sync.dma_start(out=gain_raw[:], in_=ln_g.rearrange("(p u) -> p u", u=PACK))
-        shift_raw = setup.tile([P, PACK], BF16)
-        nc.sync.dma_start(out=shift_raw[:], in_=ln_b.rearrange("(p u) -> p u", u=PACK))
-        w_raw = setup.tile([P, PACK, C_OUT], BF16)
-
-        def load_weights(b):
-            cols = slice(b * BANK, (b + 1) * BANK)
-            nc.sync.dma_start(out=w_raw[:, :, cols], in_=w_q.rearrange("(p u) c -> p u c", u=PACK)[:, :, cols])
-
-        load_weights(0)
-
         one_col = const.tile([P, 1], F32)
-        nc.vector.memset(one_col[:], 1.0)
         unread_one = const.tile([P, 1], F32)
-        nc.scalar.activation(out=unread_one[:], in_=one_col[:], func=ACT.Abs_reciprocal_sqrt)
-        small_rows = setup.tile([P, C_OUT], BF16)
-        nc.vector.memset(small_rows[:], 0.0)
-        for r, row in enumerate(rank_one_rows):
-            nc.sync.dma_start(out=small_rows[K_W + r : K_W + r + 1, :], in_=row[:, :])
-        feat_t = const.tile([P, HALF_PAIRS], F32)
-        nc.vector.memset(feat_t[K_W:P, :], 1.0)
         ident_bf = const.tile([P, P], BF16)
-        make_identity(nc, ident_bf[:])
         ident = const.tile([P, P], F32)
-        make_identity(nc, ident[:])
-
-        nc.vector.tensor_copy(out=mask_rows[:, 2, :], in_=mask_rows[:, 0, :])
-        mask_cols_ps = psum_two.tile([P, 2, P], BF16, tag="extra")
-        for m in range(2):
-            nc.tensor.transpose(
-                mask_cols_ps[:, m, :], mask_rows[:, m : m + 2, :].rearrange("p m j -> p (m j)"), ident_bf[:]
-            )
-        mask_cols = setup.tile([N_RES, 2], F32)
-        nc.vector.tensor_copy(out=mask_cols[:], in_=mask_cols_ps[0:N_RES, :, 0])
-        weights = setup.tile([N_RES, N_W, N_RES], F32)
-        for m in range(2):
-            nc.vector.scalar_tensor_tensor(
-                out=weights[:, BIASED_TERM + m, :],
-                in0=multichain[:],
-                scalar=mask_cols[:, m : m + 1],
-                in1=mask_rows[0:N_RES, m, :],
-                op0=ALU.mult,
-                op1=ALU.mult,
-            )
-        nc.vector.tensor_tensor(
-            out=weights[:, 0:BIASED_TERM, :],
-            in0=units[:],
-            in1=weights[:, BIASED_TERM : BIASED_TERM + 1, :].to_broadcast([N_RES, BIASED_TERM, N_RES]),
-            op=ALU.mult,
-        )
-        nc.sync.dma_start(out=scratch.rearrange("s (i j) -> i s j", j=N_RES), in_=weights[:])
-        load_weights(1)
-
-        cols_a = setup.tile([P, VEC_COLS], BF16)
-        cols_e = setup.tile([P, VEC_COLS], BF16)
-        nc.sync.dma_start(out=cols_a[0:N_RES, :], in_=aa_proj1[:, PLAIN_COLS:C_OUT])
-        nc.sync.dma_start(out=cols_a[N_RES:P, :], in_=aa_proj2[:, PLAIN_COLS:C_OUT])
-        nc.sync.dma_start(out=cols_e[0:N_RES, :], in_=esm_proj1[:, PLAIN_COLS:C_OUT])
-        nc.sync.dma_start(out=cols_e[N_RES:P, :], in_=esm_proj2[:, PLAIN_COLS:C_OUT])
-        for r, row in enumerate(bias_rows):
-            nc.sync.dma_start(out=small_rows[K_ONE + r : K_ONE + r + 1, :], in_=row.unsqueeze(0))
-        load_x(2)
-        load_spread(0)
-        weight_rows = setup.tile([P, P], F32)
-        nc.sync.dma_start(
-            out=weight_rows[:], in_=scratch[0 : P // TILES, :].rearrange("s (t p) -> (s t) p", p=P)
-        )
-        load_x(3)
-
-        def load_features(first_tile, tiles):
-            first = first_tile * P
-            nc.sync.dma_start(
-                out=feat_t[K_W:K_ONE, first % HALF_PAIRS : first % HALF_PAIRS + tiles * P],
-                in_=scratch[:, first : first + tiles * P],
-            )
-
-        load_features(0, HALF_TILES)
-        table_a = setup.tile([K_W, 2, PLAIN_COLS], BF16)
-        table_e = setup.tile([K_W, 2, PLAIN_COLS], BF16)
-        for tab, by_j, by_i in ((table_a, aa_proj1, aa_proj2), (table_e, esm_proj1, esm_proj2)):
-            nc.sync.dma_start(
-                out=tab[K_J : K_J + N_RES, :, :],
-                in_=by_j[:, 0:PLAIN_COLS].unsqueeze(1).to_broadcast([N_RES, 2, PLAIN_COLS]),
-            )
-            nc.sync.dma_start(
-                out=tab[K_I : K_I + I_HALF, :, :], in_=by_i.rearrange("(s m) c -> m s c", s=2)[:, :, 0:PLAIN_COLS]
-            )
-        load_act(0)
-        load_x(4)
-        load_act(1)
-        load_spread(1)
-        load_x(5)
-        load_act(2)
-        load_x(6)
-
+        feat_t = const.tile([P, HALF_PAIRS], F32)
         vec_cols = const.tile([P, 2 * PACK], F32)
-        nc.vector.tensor_copy(out=vec_cols[:, 0:PACK], in_=gain_raw[:])
-        nc.vector.tensor_copy(out=vec_cols[:, PACK : 2 * PACK], in_=shift_raw[:])
-        nc.vector.tensor_copy(
-            out=feat_t[K_J : K_J + N_RES, :].rearrange("k (i j) -> k i j", j=N_RES),
-            in_=ident[0:N_RES, 0:N_RES].unsqueeze(1).to_broadcast([N_RES, I_HALF, N_RES]),
-        )
-
-        def one_hot_i(q):
-            i_cols = slice(K_I + q * 8, K_I + (q + 1) * 8)
-            nc.gpsimd.tensor_scalar(
-                out=feat_t[K_I : K_I + I_HALF, q * GROUP : (q + 1) * GROUP].rearrange("k (i j) -> k i j", j=N_RES),
-                in0=ident[K_I : K_I + I_HALF, i_cols].unsqueeze(2).to_broadcast([I_HALF, 8, N_RES]),
-                scalar1=1.0,
-                scalar2=0.0,
-                op0=ALU.mult,
-                op1=ALU.add,
-            )
-
-        one_hot_i(0)
 
         stats = {}
         x_hats = {}
@@ -367,17 +245,18 @@ def tile_templatepairembeddermultimer_pa_t_kernel(
             products[t, bank] = product
 
         def spread_weights(term, first_pair, pairs):
-            g, offset = divmod(first_pair, GROUP)
+            g, offset = divmod(first_pair, PAIR_COLS)
             return spread_tiles[g][:, term - SPREAD_FIRST, offset : offset + pairs]
 
-        def pool_term(pair, chunks):
+        def pool_term(pair, chunks, only_half=None):
+            cols = slice(0, PAIR_COLS) if only_half is None else slice(only_half * P, (only_half + 1) * P)
             if pair not in pool_sums:
                 pool_sum = work.tile([P, VEC_CHUNKS, PAIR_COLS], F32)
                 pool_sums[pair] = pool_sum
             for c in chunks:
                 nc.gpsimd.tensor_scalar(
-                    out=pool_sums[pair][:, c, :],
-                    in0=spread_weights(POOL_TERM, pair * PAIR_COLS, PAIR_COLS),
+                    out=pool_sums[pair][:, c, cols],
+                    in0=spread_weights(POOL_TERM, pair * PAIR_COLS + cols.start, cols.stop - cols.start),
                     scalar1=w_cols[:, c, POOL_TERM : POOL_TERM + 1],
                     scalar2=0.0,
                     op0=ALU.mult,
@@ -447,6 +326,8 @@ def tile_templatepairembeddermultimer_pa_t_kernel(
 
         def small_terms_second(t):
             sum_chunks(t, (1, 0))
+
+        def project_both(t):
             for bank in range(BANKS):
                 project(t, BANKS - 1 - bank)
 
@@ -491,17 +372,41 @@ def tile_templatepairembeddermultimer_pa_t_kernel(
                 op1=ALU.add,
             )
 
-        def combine_close(t):
-            nc.gpsimd.tensor_tensor(
-                out=results[t][:, PLAIN_COLS:C_OUT], in0=results[t][:, PLAIN_COLS:C_OUT], in1=partials[t][:], op=ALU.add
+        def combine_close(t, engine, first, last):
+            engine.tensor_tensor(
+                out=results[t][:, first:last],
+                in0=results[t][:, first:last],
+                in1=partials[t][:, first - PLAIN_COLS : last - PLAIN_COLS],
+                op=ALU.add,
             )
 
-        def store(t):
-            nc.sync.dma_start(out=out_rows[t * P : (t + 1) * P, :], in_=results[t][:])
+        def store(t, first, last):
+            nc.sync.dma_start(out=out_rows[t * P : (t + 1) * P, first:last], in_=results[t][:, first:last])
+
+        def finish(t):
+            combine_close(t, nc.gpsimd, PLAIN_COLS, C_OUT)
+            store(t, 0, C_OUT)
+
+        def finish_last(t):
+            store(t, 0, PLAIN_COLS)
+            for first in (PLAIN_COLS, C_OUT - VEC_COLS // 2):
+                combine_close(t, nc.vector, first, first + VEC_COLS // 2)
+                store(t, first, first + VEC_COLS // 2)
 
         def each(stage, t):
             if 0 <= t < TILES:
                 stage(t)
+
+        every_chunk = (4, 3, 2, 1, 0)
+        row_tiles = setup.tile([P, 2, C_OUT], BF16)
+        w_raws = {}
+
+        def load_weights(b):
+            w_raw = setup.tile([P, PACK, BANK], BF16, tag="w_raw%d" % b)
+            nc.sync.dma_start(
+                out=w_raw[:], in_=w_q.rearrange("(p u) c -> p u c", u=PACK)[:, :, b * BANK : (b + 1) * BANK]
+            )
+            w_raws[b] = w_raw
 
         w_grouped = setup.tile([P, C_OUT, PACK], BF16, align_bytes=64)
 
@@ -509,7 +414,7 @@ def tile_templatepairembeddermultimer_pa_t_kernel(
             cols = slice(b * BANK, (b + 1) * BANK)
             nc.vector.tensor_copy(
                 out=w_grouped[:, cols, :].rearrange("p (c i) u -> p c u i", i=4),
-                in_=w_raw[:, :, cols].rearrange("p u (c i) -> p c u i", i=4),
+                in_=w_raws[b][:].rearrange("p u (c i) -> p c u i", i=4),
             )
 
         def quantise_weights(b):
@@ -533,24 +438,23 @@ def tile_templatepairembeddermultimer_pa_t_kernel(
         def residue_tables_copy(cols_t):
             for chunks in (slice(0, 4), slice(4, 5)):
                 n_chunks = chunks.stop - chunks.start
-                nc.scalar.copy(
+                nc.vector.tensor_copy(
                     out=a_twice[:, chunks, :, :],
                     in_=cols_t[:, chunks, 0:N_RES].unsqueeze(2).to_broadcast([P, n_chunks, 2, N_RES]),
                 )
 
-        def channel_tables(cols_t):
-            small_t = psum_two.tile([P, VEC_CHUNKS, P], BF16, tag="extra")
+        def transpose_rows(b):
+            rows_t = psum_two.tile([P, VEC_CHUNKS, P], BF16, tag="extra")
             for c in range(VEC_CHUNKS):
                 nc.tensor.transpose(
-                    small_t[:, c, :], small_rows[:, PLAIN_COLS + c * P : PLAIN_COLS + (c + 1) * P], ident_bf[:]
+                    rows_t[:, c, :], row_tiles[:, b, PLAIN_COLS + c * P : PLAIN_COLS + (c + 1) * P], ident_bf[:]
                 )
-            nc.vector.tensor_copy(out=w_cols_bf[:], in_=small_t[:, :, K_W : K_W + 2])
-            nc.vector.reduce_sum(out=bias_sums[:], in_=small_t[:, :, K_ONE:K_END], axis=mybir.AxisListType.X)
-            nc.vector.tensor_copy(out=w_cols[:], in_=small_t[:, :, K_W:K_ONE])
-            for c in range(VEC_CHUNKS):
-                nc.scalar.activation(
-                    out=b_cols[:, c, :], in_=cols_t[:, c, N_RES:P], func=ACT.Identity, bias=bias_sums[:, c : c + 1]
-                )
+            return rows_t
+
+        def rank_one_tables():
+            rows_t = transpose_rows(0)
+            nc.vector.tensor_copy(out=w_cols_bf[:], in_=rows_t[:, :, K_W : K_W + 2])
+            nc.vector.tensor_copy(out=w_cols[:], in_=rows_t[:, :, K_W:K_ONE])
             open_row_ps = psum_two.tile([P, VEC_COLS], BF16, tag="extra")
             for c in range(VEC_CHUNKS):
                 for term, row in ((OPEN_TERM, open_row_ps), (CHAIN_TERM, chain_row)):
@@ -559,16 +463,55 @@ def tile_templatepairembeddermultimer_pa_t_kernel(
                     )
             return open_row_ps
 
+        def bias_tables(cols_t):
+            rows_t = transpose_rows(1)
+            nc.vector.reduce_sum(out=bias_sums[:], in_=rows_t[:, :, K_ONE:K_END], axis=mybir.AxisListType.X)
+            for c in range(VEC_CHUNKS):
+                nc.scalar.activation(
+                    out=b_cols[:, c, :], in_=cols_t[:, c, N_RES:P], func=ACT.Identity, bias=bias_sums[:, c : c + 1]
+                )
+
         def weight_columns():
             weight_cols_ps = psum_two.tile([P, P], F32, tag="extra")
             nc.tensor.transpose(weight_cols_ps[:], weight_rows[:], ident[:])
             nc.vector.tensor_copy(out=weight_cols[:], in_=weight_cols_ps[:])
 
-        def plain_table():
-            nc.vector.tensor_tensor(out=table[0:K_W, :, :], in0=table_a[:], in1=table_e[:], op=ALU.add)
-            nc.vector.tensor_copy(
-                out=table[K_W:P, :, :],
-                in_=small_rows[K_W:P, 0:PLAIN_COLS].unsqueeze(1).to_broadcast([P - K_W, 2, PLAIN_COLS]),
+        def plain_table(s):
+            nc.vector.tensor_tensor(out=table[0:K_W, s, :], in0=table_a[:, s, :], in1=table_e[:, s, :], op=ALU.add)
+            nc.vector.tensor_tensor(
+                out=table[K_W:P, s, :],
+                in0=row_tiles[K_W:P, 0, 0:PLAIN_COLS],
+                in1=row_tiles[K_W:P, 1, 0:PLAIN_COLS],
+                op=ALU.add,
+            )
+
+        def load_features(first_tile, tiles):
+            first = first_tile * P
+            nc.sync.dma_start(
+                out=feat_t[K_W:K_ONE, first % HALF_PAIRS : first % HALF_PAIRS + tiles * P],
+                in_=scratch[:, first : first + tiles * P],
+            )
+
+        def ones_features(part):
+            cols = slice(part * HALF_PAIRS // 2, (part + 1) * HALF_PAIRS // 2)
+            nc.scalar.copy(out=feat_t[K_W:P, cols], in_=one_col[K_W:P, :].to_broadcast([P - K_W, HALF_PAIRS // 2]))
+
+        def one_hot_j(part):
+            cols = slice(part * HALF_PAIRS // 2, (part + 1) * HALF_PAIRS // 2)
+            nc.scalar.copy(
+                out=feat_t[K_J : K_J + N_RES, cols].rearrange("k (i j) -> k i j", j=N_RES),
+                in_=ident[0:N_RES, 0:N_RES].unsqueeze(1).to_broadcast([N_RES, I_HALF // 2, N_RES]),
+            )
+
+        def one_hot_i(q):
+            i_cols = slice(K_I + q * 8, K_I + (q + 1) * 8)
+            nc.gpsimd.tensor_scalar(
+                out=feat_t[K_I : K_I + I_HALF, q * 8 * N_RES : (q + 1) * 8 * N_RES].rearrange("k (i j) -> k i j", j=N_RES),
+                in0=ident[K_I : K_I + I_HALF, i_cols].unsqueeze(2).to_broadcast([I_HALF, 8, N_RES]),
+                scalar1=1.0,
+                scalar2=0.0,
+                op0=ALU.mult,
+                op1=ALU.add,
             )
 
         def first_scalar_term():
@@ -583,59 +526,162 @@ def tile_templatepairembeddermultimer_pa_t_kernel(
                 )
             scalar_sums[0] = scalar_sum
 
-        every_chunk = (4, 3, 2, 1, 0)
+        mask_rows = setup.tile([P, 3, N_RES], BF16)
+        for m, mask in enumerate((backbone_mask, pseudo_beta_mask)):
+            nc.sync.dma_start(out=mask_rows[:, m, :], in_=mask.partition_broadcast(P))
+        multichain = setup.tile([N_RES, N_RES], BF16)
+        nc.sync.dma_start(out=multichain[:], in_=multichain_mask_2d[:, :])
+        units = setup.tile([N_RES, 3, N_RES], BF16)
+        for u, unit in enumerate((unit_x, unit_y, unit_z)):
+            nc.sync.dma_start(out=units[:, u, :], in_=unit[:, :])
+        load_x(0)
+        load_x(1)
+        gain_raw = setup.tile([P, PACK], BF16)
+        nc.sync.dma_start(out=gain_raw[:], in_=ln_g.rearrange("(p u) -> p u", u=PACK))
+        shift_raw = setup.tile([P, PACK], BF16)
+        nc.sync.dma_start(out=shift_raw[:], in_=ln_b.rearrange("(p u) -> p u", u=PACK))
+        load_weights(0)
+        load_x(2)
+
+        nc.vector.memset(one_col[:], 1.0)
+        nc.scalar.activation(out=unread_one[:], in_=one_col[:], func=ACT.Abs_reciprocal_sqrt)
+        make_identity(nc, ident_bf[:])
+        make_identity(nc, ident[:])
+        for b in range(2):
+            nc.vector.memset(row_tiles[:, b, :], 0.0)
+        for r, row in enumerate(rank_one_rows):
+            nc.sync.dma_start(out=row_tiles[K_W + r : K_W + r + 1, 0, :], in_=row[:, :])
+        ones_features(0)
+
+        nc.vector.tensor_copy(out=mask_rows[:, 2, :], in_=mask_rows[:, 0, :])
+        mask_cols_ps = psum_two.tile([P, 2, P], BF16, tag="extra")
+        for m in range(2):
+            nc.tensor.transpose(
+                mask_cols_ps[:, m, :], mask_rows[:, m : m + 2, :].rearrange("p m j -> p (m j)"), ident_bf[:]
+            )
+        mask_cols = setup.tile([N_RES, 2], F32)
+        nc.vector.tensor_copy(out=mask_cols[:], in_=mask_cols_ps[0:N_RES, :, 0])
+        weights = setup.tile([N_RES, N_W, N_RES], F32)
+        for m in range(2):
+            nc.vector.scalar_tensor_tensor(
+                out=weights[:, BIASED_TERM + m, :],
+                in0=multichain[:],
+                scalar=mask_cols[:, m : m + 1],
+                in1=mask_rows[0:N_RES, m, :],
+                op0=ALU.mult,
+                op1=ALU.mult,
+            )
+        nc.vector.tensor_tensor(
+            out=weights[:, 0:BIASED_TERM, :],
+            in0=units[:],
+            in1=weights[:, BIASED_TERM : BIASED_TERM + 1, :].to_broadcast([N_RES, BIASED_TERM, N_RES]),
+            op=ALU.mult,
+        )
+        nc.sync.dma_start(out=scratch.rearrange("s (i j) -> i s j", j=N_RES), in_=weights[:])
+        cols_a = setup.tile([P, VEC_COLS], BF16)
+        cols_e = setup.tile([P, VEC_COLS], BF16)
+        nc.sync.dma_start(out=cols_a[0:N_RES, :], in_=aa_proj1[:, PLAIN_COLS:C_OUT])
+        nc.sync.dma_start(out=cols_a[N_RES:P, :], in_=aa_proj2[:, PLAIN_COLS:C_OUT])
+        nc.sync.dma_start(out=cols_e[0:N_RES, :], in_=esm_proj1[:, PLAIN_COLS:C_OUT])
+        nc.sync.dma_start(out=cols_e[N_RES:P, :], in_=esm_proj2[:, PLAIN_COLS:C_OUT])
+        load_x(3)
+        load_weights(1)
+        for r, row in enumerate(bias_rows):
+            nc.sync.dma_start(out=row_tiles[K_ONE + r : K_ONE + r + 1, 1, :], in_=row.unsqueeze(0))
+        load_spread(0)
+        weight_rows = setup.tile([P, P], F32)
+        nc.sync.dma_start(out=weight_rows[:], in_=scratch[0 : P // TILES, :].rearrange("s (t p) -> (s t) p", p=P))
+        load_features(0, HALF_TILES // 2)
+        load_spread(1)
+        table_a = setup.tile([K_W, 2, PLAIN_COLS], BF16)
+        table_e = setup.tile([K_W, 2, PLAIN_COLS], BF16)
+        for tab, by_j, by_i in ((table_a, aa_proj1, aa_proj2), (table_e, esm_proj1, esm_proj2)):
+            nc.sync.dma_start(
+                out=tab[K_J : K_J + N_RES, :, :],
+                in_=by_j[:, 0:PLAIN_COLS].unsqueeze(1).to_broadcast([N_RES, 2, PLAIN_COLS]),
+            )
+            nc.sync.dma_start(
+                out=tab[K_I : K_I + I_HALF, :, :], in_=by_i.rearrange("(s m) c -> m s c", s=2)[:, :, 0:PLAIN_COLS]
+            )
+        load_act(0)
+        load_x(4)
+        load_act(1)
+        load_spread(2)
+        load_spread(3)
+        load_x(5)
+        load_act(2)
+        load_x(6)
+
+        for q in range(4):
+            one_hot_i(q)
         ln_sum(0)
         ln_var(0)
         ln_sum(1)
         ln_rstd(0)
         ln_norm(0)
         ln_transpose(0)
+        nc.vector.tensor_copy(out=vec_cols[:, 0:PACK], in_=gain_raw[:])
+        nc.vector.tensor_copy(out=vec_cols[:, PACK : 2 * PACK], in_=shift_raw[:])
         ln_var(1)
         ln_rstd(1)
-        ln_norm(1)
-        regroup_weights(0)
-        nc.vector.tensor_tensor(out=cols_sum[:], in0=cols_a[:], in1=cols_e[:], op=ALU.add)
-        cols_t = residue_tables_transpose()
-        quantise_weights(0)
-        ln_affine(0)
-        ln_transpose(1)
-        regroup_weights(1)
         ln_sum(2)
         ln_var(2)
         ln_rstd(2)
-        residue_tables_copy(cols_t)
-        ln_affine(1)
-        open_row_ps = channel_tables(cols_t)
-        quantise_weights(1)
-        regroup(0)
-        for q in range(1, 4):
-            one_hot_i(q)
-        ln_norm(2)
-        ln_transpose(2)
-        biased_term(0)
+        regroup_weights(0)
+        ln_norm(1)
+        open_row_ps = rank_one_tables()
+        quantise_weights(0)
+        ln_affine(0)
+        ln_transpose(1)
+        ln_sum(3)
+        ln_var(3)
+        ln_rstd(3)
+        nc.vector.tensor_tensor(out=cols_sum[:], in0=cols_a[:], in1=cols_e[:], op=ALU.add)
+        cols_t = residue_tables_transpose()
+        regroup_weights(1)
         nc.scalar.copy(out=open_row[:], in_=open_row_ps[:])
-        quantise(0)
+        one_hot_j(0)
+        ln_affine(1)
+        ln_norm(2)
+        residue_tables_copy(cols_t)
+        quantise_weights(1)
+        bias_tables(cols_t)
+        ln_transpose(2)
+        regroup(0)
+        biased_term(0)
         first_scalar_term()
+        quantise(0)
         weight_columns()
-        plain_table()
-        pool_term(0, every_chunk)
+        project_both(0)
+        ln_norm(3)
+        plain_table(0)
+        pool_term(0, every_chunk, 0)
+        pool_term(0, every_chunk, 1)
         regroup(1)
         ln_affine(2)
-        for n in range(-1, TILES + 1):
+
+        for n in range(-1, TILES):
             each(load_x, n + X_AHEAD)
             if n >= 0:
                 each(load_act, n + ACT_AHEAD)
-            if n >= 2 and n % GROUP_TILES == 2 and n // GROUP_TILES + 2 < PAIRS // GROUP:
-                load_spread(n // GROUP_TILES + 2)
+            if n >= 0 and n % 2 == 0 and n // 2 + 4 < TILES // 2:
+                load_spread(n // 2 + 4)
+            if n == 1:
+                ones_features(1)
+            if n == 2:
+                one_hot_j(1)
+                load_features(HALF_TILES // 2, HALF_TILES // 2)
             if n == 8 or n == 16:
                 load_features(HALF_TILES + n - 8, 8)
-            each(combine_close, n - 1)
-            each(store, n - 1)
-            if n < 0:
-                each(ln_sum, n + 4)
-            each(ln_var, n + 4)
+            if n == 4:
+                plain_table(1)
+            if n >= 1:
+                finish(n - 1)
+            if n >= 0:
+                each(ln_var, n + 4)
             each(ln_sum, n + 5)
-            each(ln_rstd, n + 4)
+            if n >= 0:
+                each(ln_rstd, n + 4)
             each(biased_term, n + 2)
             if n % 2 == 1 and n + 3 < TILES:
                 scalar_term((n + 3) // 2, every_chunk[:3])
@@ -644,8 +690,7 @@ def tile_templatepairembeddermultimer_pa_t_kernel(
             each(combine_open, n)
             if n >= 0:
                 each(quantise, n + 1)
-            each(ln_norm, n + 4)
-            if n >= 0:
+                each(ln_norm, n + 4)
                 each(regroup, n + 2)
             if n >= 0:
                 each(ln_transpose, n + 3)
@@ -656,4 +701,7 @@ def tile_templatepairembeddermultimer_pa_t_kernel(
                 pool_term((n + 2) // 2, every_chunk[3:])
             each(small_terms_first, n + 1)
             each(small_terms_second, n + 1)
+            if n >= 0:
+                each(project_both, n + 1)
             each(combine_chain, n)
+        finish_last(TILES - 1)

@@ -40,6 +40,7 @@ OPEN_TERM, CHAIN_TERM, POOL_TERM, BIASED_TERM, SCALAR_TERM = range(N_W)
 SPREAD_FIRST = POOL_TERM
 N_SPREAD = N_W - SPREAD_FIRST
 
+SHARED_CHUNKS = 2
 PAIR_COLS = 2 * P
 
 X_AHEAD = 8
@@ -140,6 +141,7 @@ def tile_templatepairembeddermultimer_pa_t_kernel(
         pool_sums = {}
         biased_sums = {}
         scalar_sums = {}
+        shared_sums = {}
         extras = {}
         results = {}
         partials = {}
@@ -248,32 +250,45 @@ def tile_templatepairembeddermultimer_pa_t_kernel(
             g, offset = divmod(first_pair, PAIR_COLS)
             return spread_tiles[g][:, term - SPREAD_FIRST, offset : offset + pairs]
 
-        def pool_term(pair, chunks, only_half=None):
-            cols = slice(0, PAIR_COLS) if only_half is None else slice(only_half * P, (only_half + 1) * P)
-            if pair not in pool_sums:
-                pool_sum = work.tile([P, VEC_CHUNKS, PAIR_COLS], F32)
-                pool_sums[pair] = pool_sum
+        def new_pair(pair):
+            pool_sum = work.tile([P, VEC_CHUNKS, PAIR_COLS], F32)
+            pool_sums[pair] = pool_sum
+            scalar_sum = work.tile([P, VEC_CHUNKS - SHARED_CHUNKS, PAIR_COLS], F32)
+            scalar_sums[pair] = scalar_sum
+            shared_sum = work.tile([P, SHARED_CHUNKS, PAIR_COLS], F32)
+            shared_sums[pair] = shared_sum
+
+        def scalar_sum_of(pair, c, cols):
+            if c < SHARED_CHUNKS:
+                return shared_sums[pair][:, c, cols]
+            return scalar_sums[pair][:, c - SHARED_CHUNKS, cols]
+
+        def multiply_on_pool(term, pair, c, out_ap, cols):
+            nc.gpsimd.tensor_scalar(
+                out=out_ap,
+                in0=spread_weights(term, pair * PAIR_COLS + cols.start, cols.stop - cols.start),
+                scalar1=w_cols[:, c, term : term + 1],
+                scalar2=0.0,
+                op0=ALU.mult,
+                op1=ALU.add,
+            )
+
+        def pool_term(pair, chunks, cols=slice(0, PAIR_COLS)):
             for c in chunks:
-                nc.gpsimd.tensor_scalar(
-                    out=pool_sums[pair][:, c, cols],
-                    in0=spread_weights(POOL_TERM, pair * PAIR_COLS + cols.start, cols.stop - cols.start),
-                    scalar1=w_cols[:, c, POOL_TERM : POOL_TERM + 1],
-                    scalar2=0.0,
-                    op0=ALU.mult,
-                    op1=ALU.add,
-                )
+                multiply_on_pool(POOL_TERM, pair, c, pool_sums[pair][:, c, cols], cols)
+                if c < SHARED_CHUNKS:
+                    multiply_on_pool(SCALAR_TERM, pair, c, scalar_sum_of(pair, c, cols), cols)
 
         def scalar_term(pair, chunks):
-            if pair not in scalar_sums:
-                scalar_sum = work.tile([P, VEC_CHUNKS, PAIR_COLS], F32)
-                scalar_sums[pair] = scalar_sum
+            cols = slice(0, PAIR_COLS)
             for c in chunks:
-                nc.scalar.activation(
-                    out=scalar_sums[pair][:, c, :],
-                    in_=spread_weights(SCALAR_TERM, pair * PAIR_COLS, PAIR_COLS),
-                    func=ACT.Identity,
-                    scale=w_cols[:, c, SCALAR_TERM : SCALAR_TERM + 1],
-                )
+                if c >= SHARED_CHUNKS:
+                    nc.scalar.activation(
+                        out=scalar_sum_of(pair, c, cols),
+                        in_=spread_weights(SCALAR_TERM, pair * PAIR_COLS, PAIR_COLS),
+                        func=ACT.Identity,
+                        scale=w_cols[:, c, SCALAR_TERM : SCALAR_TERM + 1],
+                    )
 
         def biased_term(t):
             biased_sum = work.tile([P, VEC_CHUNKS, P], F32)
@@ -295,7 +310,7 @@ def tile_templatepairembeddermultimer_pa_t_kernel(
                 summands = (
                     a_twice[:, c, :, :].rearrange("p h j -> p (h j)"),
                     pool_sums[t // 2][:, c, half],
-                    scalar_sums[t // 2][:, c, half],
+                    scalar_sum_of(t // 2, c, half),
                     biased_sums[t][:, c, :],
                 )
                 for s, summand in enumerate(summands):
@@ -492,15 +507,10 @@ def tile_templatepairembeddermultimer_pa_t_kernel(
                 in_=scratch[:, first : first + tiles * P],
             )
 
-        def ones_features(part):
-            cols = slice(part * HALF_PAIRS // 2, (part + 1) * HALF_PAIRS // 2)
-            nc.scalar.copy(out=feat_t[K_W:P, cols], in_=one_col[K_W:P, :].to_broadcast([P - K_W, HALF_PAIRS // 2]))
-
-        def one_hot_j(part):
-            cols = slice(part * HALF_PAIRS // 2, (part + 1) * HALF_PAIRS // 2)
-            nc.scalar.copy(
-                out=feat_t[K_J : K_J + N_RES, cols].rearrange("k (i j) -> k i j", j=N_RES),
-                in_=ident[0:N_RES, 0:N_RES].unsqueeze(1).to_broadcast([N_RES, I_HALF // 2, N_RES]),
+        def one_hot_j():
+            nc.vector.tensor_copy(
+                out=feat_t[K_J : K_J + N_RES, :].rearrange("k (i j) -> k i j", j=N_RES),
+                in_=ident[0:N_RES, 0:N_RES].unsqueeze(1).to_broadcast([N_RES, I_HALF, N_RES]),
             )
 
         def one_hot_i(q):
@@ -515,16 +525,18 @@ def tile_templatepairembeddermultimer_pa_t_kernel(
             )
 
         def first_scalar_term():
-            scalar_sum = work.tile([P, VEC_CHUNKS, PAIR_COLS], F32)
             for c in range(VEC_CHUNKS):
                 nc.vector.tensor_scalar(
-                    out=scalar_sum[:, c, :],
+                    out=scalar_sum_of(0, c, slice(0, PAIR_COLS)),
                     in0=spread_weights(SCALAR_TERM, 0, PAIR_COLS),
                     scalar1=w_cols[:, c, SCALAR_TERM : SCALAR_TERM + 1],
                     scalar2=None,
                     op0=ALU.mult,
                 )
-            scalar_sums[0] = scalar_sum
+
+        def first_pool_term(cols):
+            for c in every_chunk:
+                multiply_on_pool(POOL_TERM, 0, c, pool_sums[0][:, c, cols], cols)
 
         mask_rows = setup.tile([P, 3, N_RES], BF16)
         for m, mask in enumerate((backbone_mask, pseudo_beta_mask)):
@@ -545,13 +557,12 @@ def tile_templatepairembeddermultimer_pa_t_kernel(
 
         nc.vector.memset(one_col[:], 1.0)
         nc.scalar.activation(out=unread_one[:], in_=one_col[:], func=ACT.Abs_reciprocal_sqrt)
+        nc.vector.memset(feat_t[K_W:P, :], 1.0)
+        nc.gpsimd.memset(row_tiles[:].rearrange("p b c -> p (b c)").bitcast(U32), 0)
         make_identity(nc, ident_bf[:])
         make_identity(nc, ident[:])
-        for b in range(2):
-            nc.vector.memset(row_tiles[:, b, :], 0.0)
         for r, row in enumerate(rank_one_rows):
             nc.sync.dma_start(out=row_tiles[K_W + r : K_W + r + 1, 0, :], in_=row[:, :])
-        ones_features(0)
 
         nc.vector.tensor_copy(out=mask_rows[:, 2, :], in_=mask_rows[:, 0, :])
         mask_cols_ps = psum_two.tile([P, 2, P], BF16, tag="extra")
@@ -591,7 +602,7 @@ def tile_templatepairembeddermultimer_pa_t_kernel(
         load_spread(0)
         weight_rows = setup.tile([P, P], F32)
         nc.sync.dma_start(out=weight_rows[:], in_=scratch[0 : P // TILES, :].rearrange("s (t p) -> (s t) p", p=P))
-        load_features(0, HALF_TILES // 2)
+        load_features(0, HALF_TILES)
         load_spread(1)
         table_a = setup.tile([K_W, 2, PLAIN_COLS], BF16)
         table_e = setup.tile([K_W, 2, PLAIN_COLS], BF16)
@@ -614,6 +625,7 @@ def tile_templatepairembeddermultimer_pa_t_kernel(
 
         for q in range(4):
             one_hot_i(q)
+        one_hot_j()
         ln_sum(0)
         ln_var(0)
         ln_sum(1)
@@ -640,7 +652,6 @@ def tile_templatepairembeddermultimer_pa_t_kernel(
         cols_t = residue_tables_transpose()
         regroup_weights(1)
         nc.scalar.copy(out=open_row[:], in_=open_row_ps[:])
-        one_hot_j(0)
         ln_affine(1)
         ln_norm(2)
         residue_tables_copy(cols_t)
@@ -649,14 +660,15 @@ def tile_templatepairembeddermultimer_pa_t_kernel(
         ln_transpose(2)
         regroup(0)
         biased_term(0)
+        new_pair(0)
         first_scalar_term()
         quantise(0)
         weight_columns()
         project_both(0)
         ln_norm(3)
         plain_table(0)
-        pool_term(0, every_chunk, 0)
-        pool_term(0, every_chunk, 1)
+        first_pool_term(slice(0, P))
+        first_pool_term(slice(P, PAIR_COLS))
         regroup(1)
         ln_affine(2)
 
@@ -666,11 +678,6 @@ def tile_templatepairembeddermultimer_pa_t_kernel(
                 each(load_act, n + ACT_AHEAD)
             if n >= 0 and n % 2 == 0 and n // 2 + 4 < TILES // 2:
                 load_spread(n // 2 + 4)
-            if n == 1:
-                ones_features(1)
-            if n == 2:
-                one_hot_j(1)
-                load_features(HALF_TILES // 2, HALF_TILES // 2)
             if n == 8 or n == 16:
                 load_features(HALF_TILES + n - 8, 8)
             if n == 4:
@@ -684,9 +691,10 @@ def tile_templatepairembeddermultimer_pa_t_kernel(
                 each(ln_rstd, n + 4)
             each(biased_term, n + 2)
             if n % 2 == 1 and n + 3 < TILES:
-                scalar_term((n + 3) // 2, every_chunk[:3])
+                new_pair((n + 3) // 2)
+                scalar_term((n + 3) // 2, every_chunk[:2])
             if n % 2 == 0 and n + 2 < TILES:
-                scalar_term((n + 2) // 2, every_chunk[3:])
+                scalar_term((n + 2) // 2, every_chunk[2:])
             each(combine_open, n)
             if n >= 0:
                 each(quantise, n + 1)

@@ -40,7 +40,6 @@ OPEN_TERM, CHAIN_TERM, POOL_TERM, BIASED_TERM, SCALAR_TERM = range(N_W)
 SPREAD_FIRST = POOL_TERM
 N_SPREAD = N_W - SPREAD_FIRST
 
-SHARED_CHUNKS = 2
 PAIR_COLS = 2 * P
 
 X_AHEAD = 8
@@ -141,7 +140,6 @@ def tile_templatepairembeddermultimer_pa_t_kernel(
         pool_sums = {}
         biased_sums = {}
         scalar_sums = {}
-        shared_sums = {}
         extras = {}
         results = {}
         partials = {}
@@ -253,42 +251,33 @@ def tile_templatepairembeddermultimer_pa_t_kernel(
         def new_pair(pair):
             pool_sum = work.tile([P, VEC_CHUNKS, PAIR_COLS], F32)
             pool_sums[pair] = pool_sum
-            scalar_sum = work.tile([P, VEC_CHUNKS - SHARED_CHUNKS, PAIR_COLS], F32)
+            scalar_sum = work.tile([P, VEC_CHUNKS, PAIR_COLS], F32)
             scalar_sums[pair] = scalar_sum
-            shared_sum = work.tile([P, SHARED_CHUNKS, PAIR_COLS], F32)
-            shared_sums[pair] = shared_sum
 
-        def scalar_sum_of(pair, c, cols):
-            if c < SHARED_CHUNKS:
-                return shared_sums[pair][:, c, cols]
-            return scalar_sums[pair][:, c - SHARED_CHUNKS, cols]
-
-        def multiply_on_pool(term, pair, c, out_ap, cols):
-            nc.gpsimd.tensor_scalar(
-                out=out_ap,
-                in0=spread_weights(term, pair * PAIR_COLS + cols.start, cols.stop - cols.start),
-                scalar1=w_cols[:, c, term : term + 1],
-                scalar2=0.0,
-                op0=ALU.mult,
-                op1=ALU.add,
-            )
-
-        def pool_term(pair, chunks, cols=slice(0, PAIR_COLS)):
+        def pool_term(pair, chunks, zero, cols=slice(0, PAIR_COLS)):
             for c in chunks:
-                multiply_on_pool(POOL_TERM, pair, c, pool_sums[pair][:, c, cols], cols)
-                if c < SHARED_CHUNKS:
-                    multiply_on_pool(SCALAR_TERM, pair, c, scalar_sum_of(pair, c, cols), cols)
+                nc.gpsimd.tensor_scalar(
+                    out=pool_sums[pair][:, c, cols],
+                    in0=spread_weights(POOL_TERM, pair * PAIR_COLS + cols.start, cols.stop - cols.start),
+                    scalar1=w_cols[:, c, POOL_TERM : POOL_TERM + 1],
+                    scalar2=zero,
+                    op0=ALU.mult,
+                    op1=ALU.add,
+                )
 
         def scalar_term(pair, chunks):
-            cols = slice(0, PAIR_COLS)
             for c in chunks:
-                if c >= SHARED_CHUNKS:
-                    nc.scalar.activation(
-                        out=scalar_sum_of(pair, c, cols),
-                        in_=spread_weights(SCALAR_TERM, pair * PAIR_COLS, PAIR_COLS),
-                        func=ACT.Identity,
-                        scale=w_cols[:, c, SCALAR_TERM : SCALAR_TERM + 1],
-                    )
+                nc.scalar.activation(
+                    out=scalar_sums[pair][:, c, :],
+                    in_=spread_weights(SCALAR_TERM, pair * PAIR_COLS, PAIR_COLS),
+                    func=ACT.Identity,
+                    scale=w_cols[:, c, SCALAR_TERM : SCALAR_TERM + 1],
+                )
+
+        def shared_port_free():
+            zero_col = stat_pool.tile([P, 1], F32)
+            nc.vector.memset(zero_col[:], 0.0)
+            return zero_col[:]
 
         def biased_term(t):
             biased_sum = work.tile([P, VEC_CHUNKS, P], F32)
@@ -310,7 +299,7 @@ def tile_templatepairembeddermultimer_pa_t_kernel(
                 summands = (
                     a_twice[:, c, :, :].rearrange("p h j -> p (h j)"),
                     pool_sums[t // 2][:, c, half],
-                    scalar_sum_of(t // 2, c, half),
+                    scalar_sums[t // 2][:, c, half],
                     biased_sums[t][:, c, :],
                 )
                 for s, summand in enumerate(summands):
@@ -527,16 +516,12 @@ def tile_templatepairembeddermultimer_pa_t_kernel(
         def first_scalar_term():
             for c in range(VEC_CHUNKS):
                 nc.vector.tensor_scalar(
-                    out=scalar_sum_of(0, c, slice(0, PAIR_COLS)),
+                    out=scalar_sums[0][:, c, :],
                     in0=spread_weights(SCALAR_TERM, 0, PAIR_COLS),
                     scalar1=w_cols[:, c, SCALAR_TERM : SCALAR_TERM + 1],
                     scalar2=None,
                     op0=ALU.mult,
                 )
-
-        def first_pool_term(cols):
-            for c in every_chunk:
-                multiply_on_pool(POOL_TERM, 0, c, pool_sums[0][:, c, cols], cols)
 
         mask_rows = setup.tile([P, 3, N_RES], BF16)
         for m, mask in enumerate((backbone_mask, pseudo_beta_mask)):
@@ -667,8 +652,8 @@ def tile_templatepairembeddermultimer_pa_t_kernel(
         project_both(0)
         ln_norm(3)
         plain_table(0)
-        first_pool_term(slice(0, P))
-        first_pool_term(slice(P, PAIR_COLS))
+        pool_term(0, every_chunk, 0.0, slice(0, P))
+        pool_term(0, every_chunk, 0.0, slice(P, PAIR_COLS))
         regroup(1)
         ln_affine(2)
 
@@ -692,9 +677,9 @@ def tile_templatepairembeddermultimer_pa_t_kernel(
             each(biased_term, n + 2)
             if n % 2 == 1 and n + 3 < TILES:
                 new_pair((n + 3) // 2)
-                scalar_term((n + 3) // 2, every_chunk[:2])
+                scalar_term((n + 3) // 2, every_chunk[:3])
             if n % 2 == 0 and n + 2 < TILES:
-                scalar_term((n + 2) // 2, every_chunk[2:])
+                scalar_term((n + 2) // 2, every_chunk[3:])
             each(combine_open, n)
             if n >= 0:
                 each(quantise, n + 1)
@@ -704,9 +689,9 @@ def tile_templatepairembeddermultimer_pa_t_kernel(
                 each(ln_transpose, n + 3)
                 each(ln_affine, n + 3)
             if n % 2 == 1 and n + 3 < TILES:
-                pool_term((n + 3) // 2, every_chunk[:3])
+                pool_term((n + 3) // 2, every_chunk[:3], shared_port_free())
             if n % 2 == 0 and n + 2 < TILES:
-                pool_term((n + 2) // 2, every_chunk[3:])
+                pool_term((n + 2) // 2, every_chunk[3:], shared_port_free())
             each(small_terms_first, n + 1)
             each(small_terms_second, n + 1)
             if n >= 0:

@@ -41,9 +41,10 @@ SPREAD_FIRST = POOL_TERM
 N_SPREAD = N_W - SPREAD_FIRST
 
 PAIR_COLS = 2 * P
+SPREAD_LOADS = (1, 3, 4, 4, 4)
 
 X_AHEAD = 8
-ACT_AHEAD = 3
+ACT_AHEAD = 6
 
 FLOPS = 2 * N_RES * N_RES * C_IN * C_OUT
 
@@ -95,9 +96,9 @@ def tile_templatepairembeddermultimer_pa_t_kernel(
         x_pool = stack.enter_context(tc.tile_pool(name="x", bufs=X_AHEAD))
         act_pool = stack.enter_context(tc.tile_pool(name="act", bufs=ACT_AHEAD + 2))
         stat_pool = stack.enter_context(tc.tile_pool(name="stat", bufs=8))
-        spread_pool = stack.enter_context(tc.tile_pool(name="spread", bufs=5))
+        spread_pool = stack.enter_context(tc.tile_pool(name="spread", bufs=3))
         work = stack.enter_context(tc.tile_pool(name="work", bufs=3))
-        res_pool = stack.enter_context(tc.tile_pool(name="res", bufs=4))
+        res_pool = stack.enter_context(tc.tile_pool(name="res", bufs=5))
         psum_two = stack.enter_context(tc.psum_pool(name="psum_two", bufs=2))
         psum_one = stack.enter_context(tc.psum_pool(name="psum_one", bufs=1))
 
@@ -116,12 +117,12 @@ def tile_templatepairembeddermultimer_pa_t_kernel(
             act_tiles[t] = act_tile
 
         def load_spread(g):
-            spread = spread_pool.tile([P, N_SPREAD, PAIR_COLS], F32)
-            nc.sync.dma_start(
-                out=spread[:],
-                in_=scratch[SPREAD_FIRST:N_W, g * PAIR_COLS : (g + 1) * PAIR_COLS].partition_broadcast(P),
-            )
-            spread_tiles[g] = spread
+            first_pair = sum(SPREAD_LOADS[:g])
+            first, last = first_pair * PAIR_COLS, (first_pair + SPREAD_LOADS[g]) * PAIR_COLS
+            spread = spread_pool.tile([P, N_SPREAD, last - first], F32)
+            nc.sync.dma_start(out=spread[:], in_=scratch[SPREAD_FIRST:N_W, first:last].partition_broadcast(P))
+            for pair in range(SPREAD_LOADS[g]):
+                spread_tiles[first_pair + pair] = spread[:, :, pair * PAIR_COLS : (pair + 1) * PAIR_COLS]
 
         one_col = const.tile([P, 1], F32)
         unread_one = const.tile([P, 1], F32)
@@ -254,13 +255,13 @@ def tile_templatepairembeddermultimer_pa_t_kernel(
             scalar_sum = work.tile([P, VEC_CHUNKS, PAIR_COLS], F32)
             scalar_sums[pair] = scalar_sum
 
-        def pool_term(pair, chunks, zero, cols=slice(0, PAIR_COLS)):
+        def pool_term(pair, chunks, cols=slice(0, PAIR_COLS)):
             for c in chunks:
                 nc.gpsimd.tensor_scalar(
                     out=pool_sums[pair][:, c, cols],
                     in0=spread_weights(POOL_TERM, pair * PAIR_COLS + cols.start, cols.stop - cols.start),
                     scalar1=w_cols[:, c, POOL_TERM : POOL_TERM + 1],
-                    scalar2=zero,
+                    scalar2=0.0,
                     op0=ALU.mult,
                     op1=ALU.add,
                 )
@@ -273,11 +274,6 @@ def tile_templatepairembeddermultimer_pa_t_kernel(
                     func=ACT.Identity,
                     scale=w_cols[:, c, SCALAR_TERM : SCALAR_TERM + 1],
                 )
-
-        def shared_port_free():
-            zero_col = stat_pool.tile([P, 1], F32)
-            nc.vector.memset(zero_col[:], 0.0)
-            return zero_col[:]
 
         def biased_term(t):
             biased_sum = work.tile([P, VEC_CHUNKS, P], F32)
@@ -588,7 +584,6 @@ def tile_templatepairembeddermultimer_pa_t_kernel(
         weight_rows = setup.tile([P, P], F32)
         nc.sync.dma_start(out=weight_rows[:], in_=scratch[0 : P // TILES, :].rearrange("s (t p) -> (s t) p", p=P))
         load_features(0, HALF_TILES)
-        load_spread(1)
         table_a = setup.tile([K_W, 2, PLAIN_COLS], BF16)
         table_e = setup.tile([K_W, 2, PLAIN_COLS], BF16)
         for tab, by_j, by_i in ((table_a, aa_proj1, aa_proj2), (table_e, esm_proj1, esm_proj2)):
@@ -599,14 +594,15 @@ def tile_templatepairembeddermultimer_pa_t_kernel(
             nc.sync.dma_start(
                 out=tab[K_I : K_I + I_HALF, :, :], in_=by_i.rearrange("(s m) c -> m s c", s=2)[:, :, 0:PLAIN_COLS]
             )
-        load_act(0)
         load_x(4)
+        load_act(0)
+        load_spread(1)
         load_act(1)
-        load_spread(2)
-        load_spread(3)
         load_x(5)
         load_act(2)
         load_x(6)
+        for t in range(3, ACT_AHEAD):
+            load_act(t)
 
         for q in range(4):
             one_hot_i(q)
@@ -652,8 +648,8 @@ def tile_templatepairembeddermultimer_pa_t_kernel(
         project_both(0)
         ln_norm(3)
         plain_table(0)
-        pool_term(0, every_chunk, 0.0, slice(0, P))
-        pool_term(0, every_chunk, 0.0, slice(P, PAIR_COLS))
+        pool_term(0, every_chunk, slice(0, P))
+        pool_term(0, every_chunk, slice(P, PAIR_COLS))
         regroup(1)
         ln_affine(2)
 
@@ -661,8 +657,8 @@ def tile_templatepairembeddermultimer_pa_t_kernel(
             each(load_x, n + X_AHEAD)
             if n >= 0:
                 each(load_act, n + ACT_AHEAD)
-            if n >= 0 and n % 2 == 0 and n // 2 + 4 < TILES // 2:
-                load_spread(n // 2 + 4)
+            if n in (0, 6, 12):
+                load_spread(2 + n // 6)
             if n == 8 or n == 16:
                 load_features(HALF_TILES + n - 8, 8)
             if n == 4:
@@ -689,9 +685,9 @@ def tile_templatepairembeddermultimer_pa_t_kernel(
                 each(ln_transpose, n + 3)
                 each(ln_affine, n + 3)
             if n % 2 == 1 and n + 3 < TILES:
-                pool_term((n + 3) // 2, every_chunk[:3], shared_port_free())
+                pool_term((n + 3) // 2, every_chunk[:3])
             if n % 2 == 0 and n + 2 < TILES:
-                pool_term((n + 2) // 2, every_chunk[3:], shared_port_free())
+                pool_term((n + 2) // 2, every_chunk[3:])
             each(small_terms_first, n + 1)
             each(small_terms_second, n + 1)
             if n >= 0:

from contextlib import ExitStack

import concourse.mybir as mybir
from concourse.masks import make_identity

F32 = mybir.dt.float32
BF16 = mybir.dt.bfloat16
U32 = mybir.dt.uint32
U8 = mybir.dt.uint8
FP8X4 = mybir.dt.float8_e4m3fn_x4
ALU = mybir.AluOpType
ACT = mybir.ActivationFunctionType

P = 128
N_RES = 64
PAIRS = N_RES * N_RES
C_IN = 512
C_OUT = 1024
PACK = 4
TILES = PAIRS // P
BANK = 512
BANKS = C_OUT // BANK
LN_EPS = 1e-5

PLAIN_COLS = 384
VEC_COLS = C_OUT - PLAIN_COLS
VEC_CHUNKS = VEC_COLS // P

K_J = 0
K_I = 64
K_W = 96
K_ONE = 101
K_END = 107
N_W = K_ONE - K_W
I_HALF = N_RES // 2
HALF_TILES = TILES // 2
HALF_PAIRS = PAIRS // 2

OPEN_TERM, CHAIN_TERM, POOL_TERM, BIASED_TERM, SCALAR_TERM = range(N_W)
SPREAD_FIRST = POOL_TERM
N_SPREAD = N_W - SPREAD_FIRST

PAIR_COLS = 2 * P
SPREAD_LOADS = (1, 3, 4, 4, 4)

X_AHEAD = 8
ACT_AHEAD = 6

FLOPS = 2 * N_RES * N_RES * C_IN * C_OUT


def tile_templatepairembeddermultimer_pa_t_kernel(
    tc,
    act_dgram,
    aa_proj1,
    aa_proj2,
    esm_proj1,
    esm_proj2,
    query_embedding,
    pseudo_beta_mask,
    backbone_mask,
    multichain_mask_2d,
    unit_x,
    unit_y,
    unit_z,
    ln_g,
    ln_b,
    w_q,
    b_q,
    w_pbm,
    b_pbm,
    w_x,
    b_x,
    w_y,
    b_y,
    w_z,
    b_z,
    w_bb,
    b_bb,
    out,
):
    nc = tc.nc
    x_rows = query_embedding.flatten_outer_dims()
    act_rows = act_dgram.flatten_outer_dims()
    out_rows = out.flatten_outer_dims()
    rank_one_rows = (w_x, w_y, w_z, w_bb, w_pbm)
    bias_rows = (b_q, b_pbm, b_x, b_y, b_z, b_bb)
    scratch = out.rearrange("i j c -> (i j c)")[PAIRS * C_OUT - N_W * PAIRS : PAIRS * C_OUT].rearrange(
        "(s n) -> s n", n=PAIRS
    )

    with ExitStack() as stack:
        stack.enter_context(tc.manual_schedule())
        const = stack.enter_context(tc.tile_pool(name="const", bufs=1))
        setup = stack.enter_context(tc.tile_pool(name="setup", bufs=1))
        x_pool = stack.enter_context(tc.tile_pool(name="x", bufs=X_AHEAD))
        act_pool = stack.enter_context(tc.tile_pool(name="act", bufs=ACT_AHEAD + 2))
        stat_pool = stack.enter_context(tc.tile_pool(name="stat", bufs=8))
        spread_pool = stack.enter_context(tc.tile_pool(name="spread", bufs=3))
        work = stack.enter_context(tc.tile_pool(name="work", bufs=3))
        res_pool = stack.enter_context(tc.tile_pool(name="res", bufs=5))
        psum_two = stack.enter_context(tc.psum_pool(name="psum_two", bufs=2))
        psum_one = stack.enter_context(tc.psum_pool(name="psum_one", bufs=1))

        x_tiles = {}
        act_tiles = {}
        spread_tiles = {}

        def load_x(t):
            x_tile = x_pool.tile([P, C_IN], BF16)
            nc.sync.dma_start(out=x_tile[:], in_=x_rows[t * P : (t + 1) * P, :])
            x_tiles[t] = x_tile

        def load_act(t):
            act_tile = act_pool.tile([P, C_OUT], BF16)
            nc.sync.dma_start(out=act_tile[:], in_=act_rows[t * P : (t + 1) * P, :])
            act_tiles[t] = act_tile

        def load_spread(g):
            first_pair = sum(SPREAD_LOADS[:g])
            first, last = first_pair * PAIR_COLS, (first_pair + SPREAD_LOADS[g]) * PAIR_COLS
            spread = spread_pool.tile([P, N_SPREAD, last - first], F32)
            nc.sync.dma_start(out=spread[:], in_=scratch[SPREAD_FIRST:N_W, first:last].partition_broadcast(P))
            for pair in range(SPREAD_LOADS[g]):
                spread_tiles[first_pair + pair] = spread[:, :, pair * PAIR_COLS : (pair + 1) * PAIR_COLS]

        one_col = const.tile([P, 1], F32)
        unread_one = const.tile([P, 1], F32)
        ident_bf = const.tile([P, P], BF16)
        ident = const.tile([P, P], F32)
        feat_t = const.tile([P, HALF_PAIRS], F32)
        vec_cols = const.tile([P, 2 * PACK], F32)

        stats = {}
        x_hats = {}
        x_hat_ts = {}
        q_planes = {}
        q_groupeds = {}
        q_words = {}
        products = {}
        pool_sums = {}
        biased_sums = {}
        scalar_sums = {}
        extras = {}
        results = {}
        partials = {}

        w_codes = const.tile([P, C_OUT], U32, align_bytes=64)
        w_scales = const.tile([P, C_OUT], U8, align_bytes=64)
        a_twice = const.tile([P, VEC_CHUNKS, 2, N_RES], F32)
        b_cols = const.tile([P, VEC_CHUNKS, N_RES], F32)
        w_cols = const.tile([P, VEC_CHUNKS, N_W], F32)
        open_row = const.tile([P, VEC_COLS], BF16)
        weight_cols = const.tile([P, P], F32)
        table = const.tile([P, 2, PLAIN_COLS], F32)
        chain_row = psum_one.tile([P, VEC_COLS], BF16)

        def ln_sum(t):
            unread_sum = work.tile([P, C_IN], BF16)
            stat = stat_pool.tile([P, 4], F32)
            nc.scalar.activation(
                out=unread_sum[:], in_=x_tiles[t][:], func=ACT.Identity, scale=-1.0 / C_IN, accum_out=stat[:, 0:1]
            )
            stats[t] = stat

        def ln_var(t):
            unread_sq = work.tile([P, C_IN], BF16)
            nc.scalar.activation(
                out=unread_sq[:],
                in_=x_tiles[t][:],
                func=ACT.Square,
                bias=stats[t][:, 0:1],
                accum_out=stats[t][:, 1:2],
            )

        def ln_rstd(t):
            nc.scalar.activation(
                out=stats[t][:, 2:3],
                in_=stats[t][:, 1:2],
                func=ACT.Abs_reciprocal_sqrt,
                scale=1.0 / C_IN,
                bias=LN_EPS,
            )

        def ln_norm(t):
            x_hat = work.tile([P, PACK, P], F32)
            nc.vector.tensor_scalar(
                out=x_hat[:],
                in0=x_tiles[t][:].rearrange("r (p u) -> r u p", u=PACK),
                scalar1=stats[t][:, 0:1],
                scalar2=stats[t][:, 2:3],
                op0=ALU.add,
                op1=ALU.mult,
            )
            x_hats[t] = x_hat

        def ln_transpose(t):
            x_hat_t = psum_one.tile([P, PACK, P], F32)
            for u in range(PACK):
                nc.tensor.transpose(x_hat_t[:, u, :], x_hats[t][:, u, :], ident[:])
            x_hat_ts[t] = x_hat_t

        def ln_affine(t):
            q_plane = work.tile([P, PACK, P], BF16)
            for u in range(PACK):
                nc.scalar.activation(
                    out=q_plane[:, u, :],
                    in_=x_hat_ts[t][:, u, :],
                    func=ACT.Identity,
                    scale=vec_cols[:, u : u + 1],
                    bias=vec_cols[:, PACK + u : PACK + u + 1],
                )
            q_planes[t] = q_plane

        def regroup(t):
            q_grouped = work.tile([P, P, PACK], BF16, align_bytes=64)
            nc.vector.tensor_copy(
                out=q_grouped[:].rearrange("p (r i) u -> p r u i", i=4),
                in_=q_planes[t][:].rearrange("p u (r i) -> p r u i", i=4),
            )
            q_groupeds[t] = q_grouped

        def quantise(t):
            q_codes = work.tile([P, P], U32, align_bytes=64)
            q_scales = work.tile([P, P], U8, align_bytes=64)
            nc.vector.quantize_mx(
                out=q_codes[:].bitcast(FP8X4),
                scales=q_scales[:],
                in_=q_groupeds[t][:].rearrange("p r u -> p (r u)"),
            )
            q_words[t] = (q_codes, q_scales)

        def project(t, bank):
            q_codes, q_scales = q_words[t]
            cols = slice(bank * BANK, (bank + 1) * BANK)
            product = psum_one.tile([P, BANK], F32, tag="product%d" % bank)
            nc.tensor.matmul_mx(
                out=product[:],
                lhsT=q_codes[:].bitcast(FP8X4),
                lhsT_scale=q_scales[:],
                rhs=w_codes[:, cols].bitcast(FP8X4),
                rhs_scale=w_scales[:, cols],
                start=True,
                stop=True,
            )
            products[t, bank] = product

        def spread_weights(term, first_pair, pairs):
            g, offset = divmod(first_pair, PAIR_COLS)
            return spread_tiles[g][:, term - SPREAD_FIRST, offset : offset + pairs]

        def new_pair(pair):
            pool_sum = work.tile([P, VEC_CHUNKS, PAIR_COLS], F32)
            pool_sums[pair] = pool_sum
            scalar_sum = work.tile([P, VEC_CHUNKS, PAIR_COLS], F32)
            scalar_sums[pair] = scalar_sum

        def pool_term(pair, chunks, cols=slice(0, PAIR_COLS)):
            for c in chunks:
                nc.gpsimd.tensor_scalar(
                    out=pool_sums[pair][:, c, cols],
                    in0=spread_weights(POOL_TERM, pair * PAIR_COLS + cols.start, cols.stop - cols.start),
                    scalar1=w_cols[:, c, POOL_TERM : POOL_TERM + 1],
                    scalar2=0.0,
                    op0=ALU.mult,
                    op1=ALU.add,
                )

        def scalar_term(pair, chunks):
            for c in chunks:
                nc.scalar.activation(
                    out=scalar_sums[pair][:, c, :],
                    in_=spread_weights(SCALAR_TERM, pair * PAIR_COLS, PAIR_COLS),
                    func=ACT.Identity,
                    scale=w_cols[:, c, SCALAR_TERM : SCALAR_TERM + 1],
                )

        def biased_term(t):
            biased_sum = work.tile([P, VEC_CHUNKS, P], F32)
            for c in range(VEC_CHUNKS):
                for h in range(2):
                    i = 2 * t + h
                    nc.scalar.activation(
                        out=biased_sum[:, c, h * N_RES : (h + 1) * N_RES],
                        in_=spread_weights(BIASED_TERM, i * N_RES, N_RES),
                        func=ACT.Identity,
                        scale=w_cols[:, c, BIASED_TERM : BIASED_TERM + 1],
                        bias=b_cols[:, c, i : i + 1],
                    )
            biased_sums[t] = biased_sum

        def sum_chunks(t, chunks):
            half = slice((t % 2) * P, (t % 2 + 1) * P)
            for c in chunks:
                summands = (
                    a_twice[:, c, :, :].rearrange("p h j -> p (h j)"),
                    pool_sums[t // 2][:, c, half],
                    scalar_sums[t // 2][:, c, half],
                    biased_sums[t][:, c, :],
                )
                for s, summand in enumerate(summands):
                    nc.tensor.matmul(
                        out=extras[t][:, PLAIN_COLS + c * P : PLAIN_COLS + (c + 1) * P],
                        lhsT=summand,
                        rhs=ident[:],
                        is_transpose=True,
                        start=(s == 0),
                        stop=(s == len(summands) - 1),
                    )

        def plain_matmul(t):
            first = (t % HALF_TILES) * P
            nc.tensor.matmul(
                out=extras[t][:, 0:PLAIN_COLS],
                lhsT=feat_t[:, first : first + P],
                rhs=table[:, t // HALF_TILES, :],
                start=True,
                stop=True,
            )

        def small_terms_first(t):
            extra = psum_two.tile([P, C_OUT], F32)
            extras[t] = extra
            sum_chunks(t, (4, 3, 2))
            plain_matmul(t)

        def small_terms_second(t):
            sum_chunks(t, (1, 0))

        def project_both(t):
            for bank in range(BANKS):
                project(t, BANKS - 1 - bank)

        def weight_col(term, t):
            return weight_cols[:, term * TILES + t : term * TILES + t + 1]

        def combine_open(t):
            result = res_pool.tile([P, C_OUT], F32)
            partial = work.tile([P, VEC_COLS], F32)
            first, second = slice(0, BANK), slice(BANK, C_OUT)
            nc.vector.scalar_tensor_tensor(
                out=partial[:, BANK - PLAIN_COLS : VEC_COLS],
                in0=open_row[:, BANK - PLAIN_COLS : VEC_COLS],
                scalar=weight_col(OPEN_TERM, t),
                in1=products[t, 1][:],
                op0=ALU.mult,
                op1=ALU.add,
            )
            nc.vector.tensor_tensor(out=result[:, first], in0=act_tiles[t][:, first], in1=products[t, 0][:], op=ALU.add)
            nc.vector.tensor_tensor(out=result[:, second], in0=act_tiles[t][:, second], in1=extras[t][:, second], op=ALU.add)
            nc.vector.scalar_tensor_tensor(
                out=partial[:, 0 : BANK - PLAIN_COLS],
                in0=open_row[:, 0 : BANK - PLAIN_COLS],
                scalar=weight_col(OPEN_TERM, t),
                in1=extras[t][:, PLAIN_COLS:BANK],
                op0=ALU.mult,
                op1=ALU.add,
            )
            nc.vector.tensor_tensor(
                out=result[:, 0:PLAIN_COLS], in0=result[:, 0:PLAIN_COLS], in1=extras[t][:, 0:PLAIN_COLS], op=ALU.add
            )
            results[t] = result
            partials[t] = partial

        def combine_chain(t):
            nc.vector.scalar_tensor_tensor(
                out=partials[t][:],
                in0=chain_row[:],
                scalar=weight_col(CHAIN_TERM, t),
                in1=partials[t][:],
                op0=ALU.mult,
                op1=ALU.add,
            )

        def combine_close(t, engine, first, last):
            engine.tensor_tensor(
                out=results[t][:, first:last],
                in0=results[t][:, first:last],
                in1=partials[t][:, first - PLAIN_COLS : last - PLAIN_COLS],
                op=ALU.add,
            )

        def store(t, first, last):
            nc.sync.dma_start(out=out_rows[t * P : (t + 1) * P, first:last], in_=results[t][:, first:last])

        def finish(t):
            combine_close(t, nc.gpsimd, PLAIN_COLS, C_OUT)
            store(t, 0, C_OUT)

        def finish_last(t):
            store(t, 0, PLAIN_COLS)
            for first in (PLAIN_COLS, C_OUT - VEC_COLS // 2):
                combine_close(t, nc.vector, first, first + VEC_COLS // 2)
                store(t, first, first + VEC_COLS // 2)

        def each(stage, t):
            if 0 <= t < TILES:
                stage(t)

        every_chunk = (4, 3, 2, 1, 0)
        row_tiles = setup.tile([P, 2, C_OUT], BF16)
        w_raws = {}

        def load_weights(b):
            w_raw = setup.tile([P, PACK, BANK], BF16, tag="w_raw%d" % b)
            nc.sync.dma_start(
                out=w_raw[:], in_=w_q.rearrange("(p u) c -> p u c", u=PACK)[:, :, b * BANK : (b + 1) * BANK]
            )
            w_raws[b] = w_raw

        w_grouped = setup.tile([P, C_OUT, PACK], BF16, align_bytes=64)

        def regroup_weights(b):
            cols = slice(b * BANK, (b + 1) * BANK)
            nc.vector.tensor_copy(
                out=w_grouped[:, cols, :].rearrange("p (c i) u -> p c u i", i=4),
                in_=w_raws[b][:].rearrange("p u (c i) -> p c u i", i=4),
            )

        def quantise_weights(b):
            cols = slice(b * BANK, (b + 1) * BANK)
            nc.vector.quantize_mx(
                out=w_codes[:, cols].bitcast(FP8X4),
                scales=w_scales[:, cols],
                in_=w_grouped[:, cols, :].rearrange("p c u -> p (c u)"),
            )

        cols_sum = setup.tile([P, VEC_COLS], F32)
        w_cols_bf = setup.tile([P, VEC_CHUNKS, 2], BF16)
        bias_sums = setup.tile([P, VEC_CHUNKS], F32)

        def residue_tables_transpose():
            cols_t = psum_two.tile([P, VEC_CHUNKS, P], F32, tag="extra")
            for c in range(VEC_CHUNKS):
                nc.tensor.transpose(cols_t[:, c, :], cols_sum[:, c * P : (c + 1) * P], ident[:])
            return cols_t

        def residue_tables_copy(cols_t):
            for chunks in (slice(0, 4), slice(4, 5)):
                n_chunks = chunks.stop - chunks.start
                nc.vector.tensor_copy(
                    out=a_twice[:, chunks, :, :],
                    in_=cols_t[:, chunks, 0:N_RES].unsqueeze(2).to_broadcast([P, n_chunks, 2, N_RES]),
                )

        def transpose_rows(b):
            rows_t = psum_two.tile([P, VEC_CHUNKS, P], BF16, tag="extra")
            for c in range(VEC_CHUNKS):
                nc.tensor.transpose(
                    rows_t[:, c, :], row_tiles[:, b, PLAIN_COLS + c * P : PLAIN_COLS + (c + 1) * P], ident_bf[:]
                )
            return rows_t

        def rank_one_tables():
            rows_t = transpose_rows(0)
            nc.vector.tensor_copy(out=w_cols_bf[:], in_=rows_t[:, :, K_W : K_W + 2])
            nc.vector.tensor_copy(out=w_cols[:], in_=rows_t[:, :, K_W:K_ONE])
            open_row_ps = psum_two.tile([P, VEC_COLS], BF16, tag="extra")
            for c in range(VEC_CHUNKS):
                for term, row in ((OPEN_TERM, open_row_ps), (CHAIN_TERM, chain_row)):
                    nc.tensor.transpose(
                        row[:, c * P : (c + 1) * P], w_cols_bf[:, c, term : term + 1].to_broadcast([P, P]), ident_bf[:]
                    )
            return open_row_ps

        def bias_tables(cols_t):
            rows_t = transpose_rows(1)
            nc.vector.reduce_sum(out=bias_sums[:], in_=rows_t[:, :, K_ONE:K_END], axis=mybir.AxisListType.X)
            for c in range(VEC_CHUNKS):
                nc.scalar.activation(
                    out=b_cols[:, c, :], in_=cols_t[:, c, N_RES:P], func=ACT.Identity, bias=bias_sums[:, c : c + 1]
                )

        def weight_columns():
            weight_cols_ps = psum_two.tile([P, P], F32, tag="extra")
            nc.tensor.transpose(weight_cols_ps[:], weight_rows[:], ident[:])
            nc.vector.tensor_copy(out=weight_cols[:], in_=weight_cols_ps[:])

        def plain_table(s):
            nc.vector.tensor_tensor(out=table[0:K_W, s, :], in0=table_a[:, s, :], in1=table_e[:, s, :], op=ALU.add)
            nc.vector.tensor_tensor(
                out=table[K_W:P, s, :],
                in0=row_tiles[K_W:P, 0, 0:PLAIN_COLS],
                in1=row_tiles[K_W:P, 1, 0:PLAIN_COLS],
                op=ALU.add,
            )

        def load_features(first_tile, tiles):
            first = first_tile * P
            nc.sync.dma_start(
                out=feat_t[K_W:K_ONE, first % HALF_PAIRS : first % HALF_PAIRS + tiles * P],
                in_=scratch[:, first : first + tiles * P],
            )

        def one_hot_j():
            nc.vector.tensor_copy(
                out=feat_t[K_J : K_J + N_RES, :].rearrange("k (i j) -> k i j", j=N_RES),
                in_=ident[0:N_RES, 0:N_RES].unsqueeze(1).to_broadcast([N_RES, I_HALF, N_RES]),
            )

        def one_hot_i(q):
            i_cols = slice(K_I + q * 8, K_I + (q + 1) * 8)
            nc.gpsimd.tensor_scalar(
                out=feat_t[K_I : K_I + I_HALF, q * 8 * N_RES : (q + 1) * 8 * N_RES].rearrange("k (i j) -> k i j", j=N_RES),
                in0=ident[K_I : K_I + I_HALF, i_cols].unsqueeze(2).to_broadcast([I_HALF, 8, N_RES]),
                scalar1=1.0,
                scalar2=0.0,
                op0=ALU.mult,
                op1=ALU.add,
            )

        def first_scalar_term():
            for c in range(VEC_CHUNKS):
                nc.vector.tensor_scalar(
                    out=scalar_sums[0][:, c, :],
                    in0=spread_weights(SCALAR_TERM, 0, PAIR_COLS),
                    scalar1=w_cols[:, c, SCALAR_TERM : SCALAR_TERM + 1],
                    scalar2=None,
                    op0=ALU.mult,
                )

        mask_rows = setup.tile([P, 3, N_RES], BF16)
        for m, mask in enumerate((backbone_mask, pseudo_beta_mask)):
            nc.sync.dma_start(out=mask_rows[:, m, :], in_=mask.partition_broadcast(P))
        multichain = setup.tile([N_RES, N_RES], BF16)
        nc.sync.dma_start(out=multichain[:], in_=multichain_mask_2d[:, :])
        units = setup.tile([N_RES, 3, N_RES], BF16)
        for u, unit in enumerate((unit_x, unit_y, unit_z)):
            nc.sync.dma_start(out=units[:, u, :], in_=unit[:, :])
        load_x(0)
        load_x(1)
        gain_raw = setup.tile([P, PACK], BF16)
        nc.sync.dma_start(out=gain_raw[:], in_=ln_g.rearrange("(p u) -> p u", u=PACK))
        shift_raw = setup.tile([P, PACK], BF16)
        nc.sync.dma_start(out=shift_raw[:], in_=ln_b.rearrange("(p u) -> p u", u=PACK))
        load_weights(0)
        load_x(2)

        nc.vector.memset(one_col[:], 1.0)
        nc.scalar.activation(out=unread_one[:], in_=one_col[:], func=ACT.Abs_reciprocal_sqrt)
        nc.vector.memset(feat_t[K_W:P, :], 1.0)
        nc.gpsimd.memset(row_tiles[:].rearrange("p b c -> p (b c)").bitcast(U32), 0)
        make_identity(nc, ident_bf[:])
        make_identity(nc, ident[:])
        for r, row in enumerate(rank_one_rows):
            nc.sync.dma_start(out=row_tiles[K_W + r : K_W + r + 1, 0, :], in_=row[:, :])

        nc.vector.tensor_copy(out=mask_rows[:, 2, :], in_=mask_rows[:, 0, :])
        mask_cols_ps = psum_two.tile([P, 2, P], BF16, tag="extra")
        for m in range(2):
            nc.tensor.transpose(
                mask_cols_ps[:, m, :], mask_rows[:, m : m + 2, :].rearrange("p m j -> p (m j)"), ident_bf[:]
            )
        mask_cols = setup.tile([N_RES, 2], F32)
        nc.vector.tensor_copy(out=mask_cols[:], in_=mask_cols_ps[0:N_RES, :, 0])
        weights = setup.tile([N_RES, N_W, N_RES], F32)
        for m in range(2):
            nc.vector.scalar_tensor_tensor(
                out=weights[:, BIASED_TERM + m, :],
                in0=multichain[:],
                scalar=mask_cols[:, m : m + 1],
                in1=mask_rows[0:N_RES, m, :],
                op0=ALU.mult,
                op1=ALU.mult,
            )
        nc.vector.tensor_tensor(
            out=weights[:, 0:BIASED_TERM, :],
            in0=units[:],
            in1=weights[:, BIASED_TERM : BIASED_TERM + 1, :].to_broadcast([N_RES, BIASED_TERM, N_RES]),
            op=ALU.mult,
        )
        nc.sync.dma_start(out=scratch.rearrange("s (i j) -> i s j", j=N_RES), in_=weights[:])
        cols_a = setup.tile([P, VEC_COLS], BF16)
        cols_e = setup.tile([P, VEC_COLS], BF16)
        nc.sync.dma_start(out=cols_a[0:N_RES, :], in_=aa_proj1[:, PLAIN_COLS:C_OUT])
        nc.sync.dma_start(out=cols_a[N_RES:P, :], in_=aa_proj2[:, PLAIN_COLS:C_OUT])
        nc.sync.dma_start(out=cols_e[0:N_RES, :], in_=esm_proj1[:, PLAIN_COLS:C_OUT])
        nc.sync.dma_start(out=cols_e[N_RES:P, :], in_=esm_proj2[:, PLAIN_COLS:C_OUT])
        load_x(3)
        load_weights(1)
        for r, row in enumerate(bias_rows):
            nc.sync.dma_start(out=row_tiles[K_ONE + r : K_ONE + r + 1, 1, :], in_=row.unsqueeze(0))
        load_spread(0)
        weight_rows = setup.tile([P, P], F32)
        nc.sync.dma_start(out=weight_rows[:], in_=scratch[0 : P // TILES, :].rearrange("s (t p) -> (s t) p", p=P))
        load_features(0, HALF_TILES)
        table_a = setup.tile([K_W, 2, PLAIN_COLS], BF16)
        table_e = setup.tile([K_W, 2, PLAIN_COLS], BF16)
        for tab, by_j, by_i in ((table_a, aa_proj1, aa_proj2), (table_e, esm_proj1, esm_proj2)):
            nc.sync.dma_start(
                out=tab[K_J : K_J + N_RES, :, :],
                in_=by_j[:, 0:PLAIN_COLS].unsqueeze(1).to_broadcast([N_RES, 2, PLAIN_COLS]),
            )
            nc.sync.dma_start(
                out=tab[K_I : K_I + I_HALF, :, :], in_=by_i.rearrange("(s m) c -> m s c", s=2)[:, :, 0:PLAIN_COLS]
            )
        load_x(4)
        load_act(0)
        load_spread(1)
        load_act(1)
        load_x(5)
        load_act(2)
        load_x(6)
        for t in range(3, ACT_AHEAD):
            load_act(t)

        for q in range(4):
            one_hot_i(q)
        one_hot_j()
        ln_sum(0)
        ln_var(0)
        ln_sum(1)
        ln_rstd(0)
        ln_norm(0)
        ln_transpose(0)
        nc.vector.tensor_copy(out=vec_cols[:, 0:PACK], in_=gain_raw[:])
        nc.vector.tensor_copy(out=vec_cols[:, PACK : 2 * PACK], in_=shift_raw[:])
        ln_var(1)
        ln_rstd(1)
        ln_sum(2)
        ln_var(2)
        ln_rstd(2)
        regroup_weights(0)
        ln_norm(1)
        open_row_ps = rank_one_tables()
        quantise_weights(0)
        ln_affine(0)
        ln_transpose(1)
        ln_sum(3)
        ln_var(3)
        ln_rstd(3)
        nc.vector.tensor_tensor(out=cols_sum[:], in0=cols_a[:], in1=cols_e[:], op=ALU.add)
        cols_t = residue_tables_transpose()
        regroup_weights(1)
        nc.scalar.copy(out=open_row[:], in_=open_row_ps[:])
        ln_affine(1)
        ln_norm(2)
        residue_tables_copy(cols_t)
        quantise_weights(1)
        bias_tables(cols_t)
        ln_transpose(2)
        regroup(0)
        biased_term(0)
        new_pair(0)
        first_scalar_term()
        quantise(0)
        weight_columns()
        project_both(0)
        ln_norm(3)
        plain_table(0)
        pool_term(0, every_chunk, slice(0, P))
        pool_term(0, every_chunk, slice(P, PAIR_COLS))
        regroup(1)
        ln_affine(2)

        for n in range(-1, TILES):
            each(load_x, n + X_AHEAD)
            if n >= 0:
                each(load_act, n + ACT_AHEAD)
            if n in (0, 6, 12):
                load_spread(2 + n // 6)
            if n == 8 or n == 16:
                load_features(HALF_TILES + n - 8, 8)
            if n == 4:
                plain_table(1)
            if n >= 1:
                finish(n - 1)
            if n >= 0:
                each(ln_var, n + 4)
            each(ln_sum, n + 5)
            if n >= 0:
                each(ln_rstd, n + 4)
            each(biased_term, n + 2)
            if n % 2 == 1 and n + 3 < TILES:
                new_pair((n + 3) // 2)
                scalar_term((n + 3) // 2, every_chunk[:3])
            if n % 2 == 0 and n + 2 < TILES:
                scalar_term((n + 2) // 2, every_chunk[3:])
            each(combine_open, n)
            if n >= 0:
                each(quantise, n + 1)
                each(ln_norm, n + 4)
                each(regroup, n + 2)
            if n >= 0:
                each(ln_transpose, n + 3)
                each(ln_affine, n + 3)
            if n % 2 == 1 and n + 3 < TILES:
                pool_term((n + 3) // 2, every_chunk[:3])
            if n % 2 == 0 and n + 2 < TILES:
                pool_term((n + 2) // 2, every_chunk[3:])
            each(small_terms_first, n + 1)
            each(small_terms_second, n + 1)
            if n >= 0:
                each(project_both, n + 1)
            each(combine_chain, n)
        finish_last(TILES - 1)
